import numpy as np
import ml_dtypes


def mxq(x, axis, fmt="e4m3"):
    dtype, down = {"e4m3": (ml_dtypes.float8_e4m3fn, 7), "e5m2": (ml_dtypes.float8_e5m2, 14)}[fmt]
    v = np.moveaxis(np.asarray(x, np.float32).astype(ml_dtypes.bfloat16).astype(np.float64), axis, -1)
    blocks = v.reshape(v.shape[:-1] + (-1, 32))
    amax = np.abs(blocks).max(-1, keepdims=True)
    byte = np.maximum(np.where(amax > 0, np.frexp(amax)[1] - 1 + 127, 0) - down, 1)
    scale = np.exp2(byte - 127.0)
    codes = (blocks / scale).astype(np.float32).astype(dtype).astype(np.float64)
    return np.moveaxis((codes * scale).reshape(v.shape), -1, axis)


WIDE = False


def mx_kscale(k):
    if not WIDE:
        return np.ones(k)
    levels = np.array([10, -10, 5, -5, 0])
    a = np.random.permutation(np.resize(levels, k // 512 * 4)).reshape(k // 512, 4)
    idx = np.arange(k)
    return np.exp2(a[idx // 512, idx % 128 // 32])


BF16 = ml_dtypes.bfloat16


def bf(x):
    return np.asarray(x, np.float32).astype(BF16)


def f64(x):
    return np.asarray(x).astype(np.float64)


B, Q, S, T, HID, NH = 1, 1024, 4, 1024, 512, 4
DH = HID // NH
EPS = 1e-12
NEG = -10000.0


def setup_inputs():
    t = mx_kscale(HID)
    sgn = np.where(np.random.standard_normal(HID) < 0.0, -1.0, 1.0)
    off = sgn * (1.0 + 0.1 * np.random.standard_normal(HID))
    return {"q": bf(np.random.standard_normal((B, Q, HID)) * 1.5),
            "k": bf(np.random.standard_normal((B, S, T, HID))),
            "v": bf((off + 0.5 * np.random.standard_normal((B, S, T, HID))) * t),
            "mask": bf(np.random.randint(0, 2, (B, S, T))),
            "Wo": bf(np.random.standard_normal((HID, HID)) / np.sqrt(HID) / t[None, :]),
            "bo": bf(0.1 + 0.1 * np.random.standard_normal(HID)),
            "gamma": bf(1.0 + 0.1 * np.random.standard_normal(HID)),
            "beta": bf(0.1 * np.random.standard_normal(HID))}


def reference(q, k, v, mask, Wo, bo, gamma, beta):
    qh = f64(q).reshape(B, Q, NH, DH).transpose(0, 2, 1, 3)[:, None]
    kh = f64(k).reshape(B, S, T, NH, DH).transpose(0, 1, 3, 4, 2)
    vh = f64(v).reshape(B, S, T, NH, DH).transpose(0, 1, 3, 2, 4)
    sc = qh @ kh * (1.0 / np.sqrt(DH)) + f64(mask)[:, :, None, None, :] * NEG
    e = np.exp(sc - sc.max(-1, keepdims=True))
    ctx = (mxq(e, 4, "e4m3") @ mxq(vh, 3, "e4m3")) / e.sum(-1, keepdims=True)
    res = ctx.transpose(0, 3, 1, 2, 4).reshape(B, Q, S, HID)
    y = (mxq(res, 3, "e4m3") @ mxq(f64(Wo), 1, "e4m3").T) + f64(bo)
    mu = y.mean(-1, keepdims=True)
    var = ((y - mu) ** 2).mean(-1, keepdims=True)
    return (y - mu) / np.sqrt(var + EPS) * f64(gamma) + f64(beta)

@@ -1,0 +1,339 @@
+from contextlib import ExitStack
+import math
+
+import concourse.mybir as mybir
+from concourse.masks import make_identity
+
+F32 = mybir.dt.float32
+BF16 = mybir.dt.bfloat16
+U32 = mybir.dt.uint32
+U8 = mybir.dt.uint8
+FP8X4 = mybir.dt.float8_e4m3fn_x4
+ALU = mybir.AluOpType
+ACT = mybir.ActivationFunctionType
+AX = mybir.AxisListType
+
+Q, S, T, HID, NH = 1024, 4, 1024, 512, 4
+DH = HID // NH
+P = 128
+PACK = 4
+K_PASS = P * PACK
+BANK = 512
+Q_TILES = Q // P
+T_TILES = T // P
+T_BANKS = T // BANK
+T_PASSES = T // K_PASS
+O_TILES = HID // P
+SCALE = 1.0 / math.sqrt(DH)
+NEG = -10000.0
+EPS = 1e-12
+
+FLOPS = 2 * S * NH * Q * T * DH * 2 + 2 * Q * S * HID * HID
+
+
+def tile_multiheadtokenattention_pa_t_kernel(tc, q, k, v, mask, Wo, bo, gamma, beta, out):
+    nc = tc.nc
+    with ExitStack() as stack:
+        consts = stack.enter_context(tc.tile_pool(name="consts", bufs=1))
+        sentence = stack.enter_context(tc.tile_pool(name="sentence", bufs=2))
+        unit_pool = stack.enter_context(tc.tile_pool(name="unit", bufs=3))
+        packed_pool = stack.enter_context(tc.tile_pool(name="packed", bufs=2 * NH))
+        block_pool = stack.enter_context(tc.tile_pool(name="block", bufs=2))
+        small = stack.enter_context(tc.tile_pool(name="small", bufs=4))
+        psum_sc = stack.enter_context(tc.psum_pool(name="psum_sc", bufs=2 * T_BANKS))
+        psum_tr = stack.enter_context(tc.psum_pool(name="psum_tr", bufs=2))
+        psum_ctx = stack.enter_context(tc.psum_pool(name="psum_ctx", bufs=1))
+        psum_y = stack.enter_context(tc.psum_pool(name="psum_y", bufs=1))
+
+        mask_rows = consts.tile([P, P], BF16)
+        nc.vector.memset(mask_rows[:], 0.0)
+        nc.sync.dma_start(
+            out=mask_rows[0 : S * T_TILES, :], in_=mask.rearrange("b s (c t) -> (b s c) t", t=P)
+        )
+        k_rows = k.rearrange("b s (n p) f -> (b s) p n f", p=P)
+        v_rows = v.rearrange("b s (j p e) f -> (b s) p j (e f)", p=P, e=2)
+        k_raw = []
+        v_raw = []
+        for s in range(S):
+            k_raw.append(consts.tile([P, T_TILES, HID], BF16, name="k_raw%d" % s))
+            v_raw.append(consts.tile([P, T // (2 * P), 2 * HID], BF16, name="v_raw%d" % s))
+        q_raw = consts.tile([P, Q_TILES, HID], BF16)
+        wo_raw = consts.tile([P, O_TILES, HID], BF16)
+        bo_all = consts.tile([P, HID], BF16)
+        gamma_all = consts.tile([P, HID], BF16)
+        beta_all = consts.tile([P, HID], BF16)
+        nc.sync.dma_start(out=k_raw[0][:], in_=k_rows[0])
+        nc.sync.dma_start(out=q_raw[:], in_=q.rearrange("b (n p) f -> p (b n) f", p=P))
+        nc.sync.dma_start(out=v_raw[0][:], in_=v_rows[0])
+        nc.sync.dma_start(out=wo_raw[:], in_=Wo.rearrange("(n p) f -> p n f", p=P))
+        nc.sync.dma_start(out=bo_all[:], in_=bo.partition_broadcast(P))
+        nc.sync.dma_start(out=gamma_all[:], in_=gamma.partition_broadcast(P))
+        nc.sync.dma_start(out=beta_all[:], in_=beta.partition_broadcast(P))
+        for s in range(1, S):
+            nc.sync.dma_start(out=k_raw[s][:], in_=k_rows[s])
+            nc.sync.dma_start(out=v_raw[s][:], in_=v_rows[s])
+
+        ident_bf = consts.tile([P, P], BF16)
+        make_identity(nc, ident_bf[:])
+        ident_f32 = consts.tile([P, P], F32)
+        make_identity(nc, ident_f32[:])
+        minus_half = consts.tile([P, 1], F32)
+        nc.vector.memset(minus_half[:], -0.5)
+
+        mask_flipped = psum_tr.tile([P, P], BF16, tag="tr")
+        nc.tensor.transpose(mask_flipped[:], mask_rows[:], ident_bf[:])
+        mask_col = consts.tile([P, S * T_TILES], F32)
+        nc.vector.tensor_scalar(
+            out=mask_col[:],
+            in0=mask_flipped[:, 0 : S * T_TILES],
+            scalar1=NEG / SCALE,
+            scalar2=None,
+            op0=ALU.mult,
+        )
+        mask_bias = consts.tile([P, S * T_TILES, P], F32)
+        nc.vector.tensor_copy(
+            out=mask_bias[:], in_=mask_col[:].unsqueeze(2).to_broadcast([P, S * T_TILES, P])
+        )
+
+        qT = consts.tile([P, NH, Q], BF16)
+
+        def transpose_queries(qt):
+            flipped = psum_tr.tile([P, NH, P], BF16, tag="tr")
+            for h in range(NH):
+                nc.tensor.transpose(
+                    flipped[:, h, :], q_raw[:, qt, h * DH : (h + 1) * DH], ident_bf[:]
+                )
+            nc.vector.tensor_copy(out=qT[:, :, qt * P : (qt + 1) * P], in_=flipped[:])
+
+        def transpose_keys(s):
+            kT = sentence.tile([P, NH, T], BF16, tag="kT")
+            for tt in range(T_TILES):
+                flipped = psum_tr.tile([P, NH, P], BF16, tag="tr")
+                for h in range(NH):
+                    nc.tensor.transpose(
+                        flipped[:, h, :], k_raw[s][:, tt, h * DH : (h + 1) * DH], ident_bf[:]
+                    )
+                nc.scalar.copy(out=kT[:, :, tt * P : (tt + 1) * P], in_=flipped[:])
+            return kT
+
+        def quantise_values(s):
+            grouped = sentence.tile([P, T_PASSES, HID, PACK], BF16, tag="v_grouped", align_bytes=64)
+            for c in range(T_PASSES):
+                nc.vector.tensor_copy(
+                    out=grouped[:, c].rearrange("p f (u e) -> p f u e", e=2),
+                    in_=v_raw[s][:, 2 * c : 2 * c + 2, :].rearrange("p u (e f) -> p f u e", e=2),
+                )
+            codes = sentence.tile([P, T_PASSES, HID], U32, tag="v_codes", align_bytes=64)
+            scales = sentence.tile([P, T_PASSES, HID], U8, tag="v_scales", align_bytes=64)
+            nc.vector.quantize_mx(
+                out=codes[:].rearrange("p c f -> p (c f)").bitcast(FP8X4),
+                scales=scales[:].rearrange("p c f -> p (c f)"),
+                in_=grouped[:].rearrange("p c f j -> p (c f j)"),
+            )
+            return codes, scales
+
+        wo_words = wo_raw[:].bitcast(F32)
+        wo_grouped = consts.tile([P, HID, PACK], BF16, align_bytes=64)
+        wo_grouped_words = wo_grouped[:].bitcast(F32)
+        for half in range(O_TILES // 2):
+            flipped = psum_tr.tile([P, 2, 2, P], F32, tag="tr")
+            for a in range(2):
+                for u in range(2):
+                    nc.tensor.transpose(
+                        flipped[:, a, u, :],
+                        wo_words[:, 2 * half + a, u * P : (u + 1) * P],
+                        ident_f32[:],
+                    )
+            nc.vector.tensor_copy(
+                out=wo_grouped_words[:, 2 * half * P : (2 * half + 2) * P, :].rearrange(
+                    "p (a o) u -> p a o u", a=2
+                ),
+                in_=flipped[:].rearrange("p a u o -> p a o u"),
+            )
+        wo_codes = consts.tile([P, HID], U32, align_bytes=64)
+        wo_scales = consts.tile([P, HID], U8, align_bytes=64)
+        nc.vector.quantize_mx(
+            out=wo_codes[:].bitcast(FP8X4),
+            scales=wo_scales[:],
+            in_=wo_grouped[:].rearrange("p o j -> p (o j)"),
+        )
+
+        def scores(s, qt, h, kT):
+            banks = []
+            for b in range(T_BANKS):
+                sc = psum_sc.tile([P, BANK], F32, tag="sc")
+                for j in range(BANK // P):
+                    nc.tensor.matmul(
+                        out=sc[:, j * P : (j + 1) * P],
+                        lhsT=mask_bias[:, s * T_TILES + b * (BANK // P) + j, :],
+                        rhs=ident_f32[:],
+                        is_transpose=True,
+                        start=(j == 0),
+                        stop=False,
+                    )
+                nc.tensor.matmul(
+                    out=sc[:],
+                    lhsT=qT[:, h, qt * P : (qt + 1) * P],
+                    rhs=kT[:, h, b * BANK : (b + 1) * BANK],
+                    start=False,
+                    stop=True,
+                )
+                banks.append(sc)
+            return banks
+
+        def softmax(banks, row_sums, h):
+            top = small.tile([P, T_BANKS], F32, tag="top")
+            for b in range(T_BANKS):
+                nc.vector.tensor_reduce(out=top[:, b : b + 1], in_=banks[b][:], axis=AX.X, op=ALU.max)
+            shift = small.tile([P, 1], F32, tag="shift")
+            nc.vector.tensor_scalar(
+                out=shift[:],
+                in0=top[:, 0:1],
+                scalar1=top[:, 1:2],
+                scalar2=-SCALE,
+                op0=ALU.max,
+                op1=ALU.mult,
+            )
+            e = unit_pool.tile([P, T], BF16, tag="e")
+            for b in range(T_BANKS):
+                nc.scalar.activation(
+                    out=e[:, b * BANK : (b + 1) * BANK],
+                    in_=banks[b][:],
+                    func=ACT.Exp,
+                    bias=shift[:],
+                    scale=SCALE,
+                    accum_out=row_sums[:, h * T_BANKS + b : h * T_BANKS + b + 1],
+                )
+            return e
+
+        def pack(e):
+            words = e[:].bitcast(F32)
+            flipped = psum_tr.tile([P, T_PASSES * 2, P], F32, tag="tr")
+            for j in range(T_PASSES * 2):
+                nc.tensor.transpose(flipped[:, j, :], words[:, j * P : (j + 1) * P], ident_f32[:])
+            grouped = unit_pool.tile([P, T_PASSES * P * PACK], BF16, tag="e_grouped", align_bytes=64)
+            nc.scalar.copy(
+                out=grouped[:].bitcast(F32).rearrange("p (c r u) -> p c r u", c=T_PASSES, u=2),
+                in_=flipped[:].rearrange("p (c u) r -> p c r u", u=2),
+            )
+            codes = packed_pool.tile([P, T_PASSES * P], U32, tag="e_codes", align_bytes=64)
+            scales = packed_pool.tile([P, T_PASSES * P], U8, tag="e_scales", align_bytes=64)
+            nc.vector.quantize_mx(out=codes[:].bitcast(FP8X4), scales=scales[:], in_=grouped[:])
+            return codes, scales
+
+        def finish_block(s, qt, packed, row_sums, v_codes, v_scales):
+            ctx_ps = psum_ctx.tile([P, HID], F32, tag="ctx")
+            for h in range(NH):
+                e_codes, e_scales = packed[h]
+                for c in range(T_PASSES):
+                    nc.tensor.matmul_mx(
+                        out=ctx_ps[:, h * DH : (h + 1) * DH],
+                        lhsT=e_codes[:, c * P : (c + 1) * P].bitcast(FP8X4),
+                        lhsT_scale=e_scales[:, c * P : (c + 1) * P],
+                        rhs=v_codes[:, c, h * DH : (h + 1) * DH].bitcast(FP8X4),
+                        rhs_scale=v_scales[:, c, h * DH : (h + 1) * DH],
+                        start=(c == 0),
+                        stop=(c == T_PASSES - 1),
+                    )
+            total = small.tile([P, NH], F32, tag="total")
+            nc.vector.tensor_reduce(
+                out=total[:],
+                in_=row_sums[:].rearrange("p (h b) -> p h b", b=T_BANKS),
+                axis=AX.X,
+                op=ALU.add,
+            )
+            inverse = small.tile([P, NH], F32, tag="inverse")
+            nc.vector.reciprocal(out=inverse[:], in_=total[:])
+            res = block_pool.tile([P, HID], BF16, tag="res")
+            nc.vector.tensor_tensor(
+                out=res[:].rearrange("p (h d) -> p h d", h=NH),
+                in0=ctx_ps[:].rearrange("p (h d) -> p h d", h=NH),
+                in1=inverse[:].unsqueeze(2).to_broadcast([P, NH, DH]),
+                op=ALU.mult,
+            )
+
+            res_words = res[:].bitcast(F32)
+            flipped = psum_tr.tile([P, 2, P], F32, tag="tr")
+            for u in range(2):
+                nc.tensor.transpose(flipped[:, u, :], res_words[:, u * P : (u + 1) * P], ident_f32[:])
+            grouped = block_pool.tile([P, P * PACK], BF16, tag="res_grouped", align_bytes=64)
+            nc.scalar.copy(
+                out=grouped[:].bitcast(F32).rearrange("p (r u) -> p r u", u=2),
+                in_=flipped[:].rearrange("p u r -> p r u"),
+            )
+            res_codes = block_pool.tile([P, P], U32, tag="res_codes", align_bytes=64)
+            res_scales = block_pool.tile([P, P], U8, tag="res_scales", align_bytes=64)
+            nc.vector.quantize_mx(out=res_codes[:].bitcast(FP8X4), scales=res_scales[:], in_=grouped[:])
+
+            y_ps = psum_y.tile([P, HID], F32, tag="y")
+            nc.tensor.matmul_mx(
+                out=y_ps[:],
+                lhsT=res_codes[:].bitcast(FP8X4),
+                lhsT_scale=res_scales[:],
+                rhs=wo_codes[:].bitcast(FP8X4),
+                rhs_scale=wo_scales[:],
+                start=True,
+                stop=True,
+            )
+
+            y = block_pool.tile([P, HID], F32, tag="y_sb")
+            y_sum = small.tile([P, 1], F32, tag="y_sum")
+            nc.vector.scalar_tensor_tensor(
+                out=y[:], in0=y_ps[:], scalar=1.0, in1=bo_all[:], op0=ALU.mult, op1=ALU.add,
+                accum_out=y_sum[:],
+            )
+            neg_mean = small.tile([P, 1], F32, tag="neg_mean")
+            nc.vector.tensor_scalar(
+                out=neg_mean[:], in0=y_sum[:], scalar1=-1.0 / HID, scalar2=None, op0=ALU.mult
+            )
+            squares = block_pool.tile([P, HID], BF16, tag="squares")
+            dev2 = small.tile([P, 1], F32, tag="dev2")
+            nc.scalar.activation(
+                out=squares[:], in_=y[:], func=ACT.Square, bias=neg_mean[:], scale=1.0,
+                accum_out=dev2[:],
+            )
+            var_eps = small.tile([P, 1], F32, tag="var_eps")
+            nc.gpsimd.tensor_scalar(
+                out=var_eps[:], in0=dev2[:], scalar1=1.0 / HID, scalar2=EPS, op0=ALU.mult, op1=ALU.add
+            )
+            rstd = small.tile([P, 1], F32, tag="rstd")
+            nc.gpsimd.tensor_tensor(out=rstd[:], in0=var_eps[:], in1=minus_half[:], op=ALU.pow)
+            centred = block_pool.tile([P, HID], F32, tag="centred")
+            nc.vector.scalar_tensor_tensor(
+                out=centred[:], in0=y[:], scalar=neg_mean[:], in1=gamma_all[:], op0=ALU.add, op1=ALU.mult
+            )
+            result = block_pool.tile([P, HID], F32, tag="result")
+            nc.vector.scalar_tensor_tensor(
+                out=result[:], in0=centred[:], scalar=rstd[:], in1=beta_all[:], op0=ALU.mult, op1=ALU.add
+            )
+            nc.sync.dma_start(out=out[0, qt * P : (qt + 1) * P, s, :], in_=result[:])
+
+        units = [(s, qt, h) for s in range(S) for qt in range(Q_TILES) for h in range(NH)]
+        kT_of = {0: transpose_keys(0)}
+        transpose_queries(0)
+        v_of = {0: quantise_values(0)}
+        banks_of = {}
+        e_of = {}
+        sums_of = {}
+        packed_of = {}
+        for step in range(len(units) + 2):
+            if step < len(units):
+                s, qt, h = units[step]
+                banks_of[step] = scores(s, qt, h, kT_of[s])
+                if s == 0 and h == 0 and qt + 1 < Q_TILES:
+                    transpose_queries(qt + 1)
+                if qt == Q_TILES // 2 and h == 0 and s + 1 < S:
+                    kT_of[s + 1] = transpose_keys(s + 1)
+                    v_of[s + 1] = quantise_values(s + 1)
+            if 1 <= step <= len(units):
+                s, qt, h = units[step - 1]
+                if h == 0:
+                    sums_of[(s, qt)] = small.tile([P, NH * T_BANKS], F32, tag="row_sums", name="row_sums")
+                e_of[step - 1] = softmax(banks_of[step - 1], sums_of[(s, qt)], h)
+            if step >= 2:
+                s, qt, h = units[step - 2]
+                packed_of[h] = pack(e_of[step - 2])
+                if h == NH - 1:
+                    finish_block(
+                        s, qt, [packed_of[i] for i in range(NH)], sums_of[(s, qt)], v_of[s][0], v_of[s][1]
+                    )

@@ -34,6 +34,7 @@ FLOPS = 2 * S * NH * Q * T * DH * 2 + 2 * Q * S * HID * HID
 def tile_multiheadtokenattention_pa_t_kernel(tc, q, k, v, mask, Wo, bo, gamma, beta, out):
     nc = tc.nc
     with ExitStack() as stack:
+        stack.enter_context(tc.manual_schedule())
         consts = stack.enter_context(tc.tile_pool(name="consts", bufs=1))
         sentence = stack.enter_context(tc.tile_pool(name="sentence", bufs=2))
         unit_pool = stack.enter_context(tc.tile_pool(name="unit", bufs=3))
@@ -64,8 +65,8 @@ def tile_multiheadtokenattention_pa_t_kernel(tc, q, k, v, mask, Wo, bo, gamma, b
         beta_all = consts.tile([P, HID], BF16)
         nc.sync.dma_start(out=k_raw[0][:], in_=k_rows[0])
         nc.sync.dma_start(out=q_raw[:], in_=q.rearrange("b (n p) f -> p (b n) f", p=P))
-        nc.sync.dma_start(out=v_raw[0][:], in_=v_rows[0])
         nc.sync.dma_start(out=wo_raw[:], in_=Wo.rearrange("(n p) f -> p n f", p=P))
+        nc.sync.dma_start(out=v_raw[0][:], in_=v_rows[0])
         nc.sync.dma_start(out=bo_all[:], in_=bo.partition_broadcast(P))
         nc.sync.dma_start(out=gamma_all[:], in_=gamma.partition_broadcast(P))
         nc.sync.dma_start(out=beta_all[:], in_=beta.partition_broadcast(P))
@@ -96,6 +97,8 @@ def tile_multiheadtokenattention_pa_t_kernel(tc, q, k, v, mask, Wo, bo, gamma, b
         )
 
         qT = consts.tile([P, NH, Q], BF16)
+        kT_of = {}
+        v_of = {}
 
         def transpose_queries(qt):
             flipped = psum_tr.tile([P, NH, P], BF16, tag="tr")
@@ -105,32 +108,39 @@ def tile_multiheadtokenattention_pa_t_kernel(tc, q, k, v, mask, Wo, bo, gamma, b
                 )
             nc.vector.tensor_copy(out=qT[:, :, qt * P : (qt + 1) * P], in_=flipped[:])
 
-        def transpose_keys(s):
-            kT = sentence.tile([P, NH, T], BF16, tag="kT")
-            for tt in range(T_TILES):
-                flipped = psum_tr.tile([P, NH, P], BF16, tag="tr")
-                for h in range(NH):
-                    nc.tensor.transpose(
-                        flipped[:, h, :], k_raw[s][:, tt, h * DH : (h + 1) * DH], ident_bf[:]
-                    )
-                nc.scalar.copy(out=kT[:, :, tt * P : (tt + 1) * P], in_=flipped[:])
-            return kT
+        def transpose_keys(s, tt):
+            if tt == 0:
+                kT_of[s] = sentence.tile([P, NH, T], BF16, tag="kT", name="kT")
+            flipped = psum_tr.tile([P, NH, P], BF16, tag="tr")
+            for h in range(NH):
+                nc.tensor.transpose(
+                    flipped[:, h, :], k_raw[s][:, tt, h * DH : (h + 1) * DH], ident_bf[:]
+                )
+            nc.scalar.copy(out=kT_of[s][:, :, tt * P : (tt + 1) * P], in_=flipped[:])
+
+        def group_values(s, c):
+            if c == 0:
+                v_of[s] = (
+                    sentence.tile([P, T_PASSES, HID, PACK], BF16, tag="v_grouped", name="v_grouped", align_bytes=64),
+                    sentence.tile([P, T_PASSES, HID], U32, tag="v_codes", name="v_codes", align_bytes=64),
+                    sentence.tile([P, T_PASSES, HID], U8, tag="v_scales", name="v_scales", align_bytes=64),
+                )
+            nc.vector.tensor_copy(
+                out=v_of[s][0][:, c].rearrange("p f (u e) -> p f u e", e=2),
+                in_=v_raw[s][:, 2 * c : 2 * c + 2, :].rearrange("p u (e f) -> p f u e", e=2),
+            )
 
         def quantise_values(s):
-            grouped = sentence.tile([P, T_PASSES, HID, PACK], BF16, tag="v_grouped", align_bytes=64)
-            for c in range(T_PASSES):
-                nc.vector.tensor_copy(
-                    out=grouped[:, c].rearrange("p f (u e) -> p f u e", e=2),
-                    in_=v_raw[s][:, 2 * c : 2 * c + 2, :].rearrange("p u (e f) -> p f u e", e=2),
-                )
-            codes = sentence.tile([P, T_PASSES, HID], U32, tag="v_codes", align_bytes=64)
-            scales = sentence.tile([P, T_PASSES, HID], U8, tag="v_scales", align_bytes=64)
+            grouped, codes, scales = v_of[s]
             nc.vector.quantize_mx(
                 out=codes[:].rearrange("p c f -> p (c f)").bitcast(FP8X4),
                 scales=scales[:].rearrange("p c f -> p (c f)"),
                 in_=grouped[:].rearrange("p c f j -> p (c f j)"),
             )
-            return codes, scales
+
+        for tt in range(T_TILES):
+            transpose_keys(0, tt)
+        transpose_queries(0)
 
         wo_words = wo_raw[:].bitcast(F32)
         wo_grouped = consts.tile([P, HID, PACK], BF16, align_bytes=64)
@@ -158,8 +168,11 @@ def tile_multiheadtokenattention_pa_t_kernel(tc, q, k, v, mask, Wo, bo, gamma, b
             in_=wo_grouped[:].rearrange("p o j -> p (o j)"),
         )
 
-        def scores(s, qt, h, kT):
-            banks = []
+        units = [(s, qt, h) for s in range(S) for qt in range(Q_TILES) for h in range(NH)]
+        live = {}
+
+        def scores(i):
+            s, qt, h = units[i]
             for b in range(T_BANKS):
                 sc = psum_sc.tile([P, BANK], F32, tag="sc")
                 for j in range(BANK // P):
@@ -174,17 +187,22 @@ def tile_multiheadtokenattention_pa_t_kernel(tc, q, k, v, mask, Wo, bo, gamma, b
                 nc.tensor.matmul(
                     out=sc[:],
                     lhsT=qT[:, h, qt * P : (qt + 1) * P],
-                    rhs=kT[:, h, b * BANK : (b + 1) * BANK],
+                    rhs=kT_of[s][:, h, b * BANK : (b + 1) * BANK],
                     start=False,
                     stop=True,
                 )
-                banks.append(sc)
-            return banks
+                live["sc", i, b] = sc
 
-        def softmax(banks, row_sums, h):
+        def bank_maxima(i):
             top = small.tile([P, T_BANKS], F32, tag="top")
             for b in range(T_BANKS):
-                nc.vector.tensor_reduce(out=top[:, b : b + 1], in_=banks[b][:], axis=AX.X, op=ALU.max)
+                nc.vector.tensor_reduce(
+                    out=top[:, b : b + 1], in_=live["sc", i, b][:], axis=AX.X, op=ALU.max
+                )
+            live["top", i] = top
+
+        def row_shift(i):
+            top = live["top", i]
             shift = small.tile([P, 1], F32, tag="shift")
             nc.vector.tensor_scalar(
                 out=shift[:],
@@ -194,20 +212,29 @@ def tile_multiheadtokenattention_pa_t_kernel(tc, q, k, v, mask, Wo, bo, gamma, b
                 op0=ALU.max,
                 op1=ALU.mult,
             )
+            live["shift", i] = shift
+
+        def exponentials(i):
+            h = units[i][2]
+            if h == 0:
+                live["row_sums", i // NH] = small.tile(
+                    [P, NH * T_BANKS], F32, tag="row_sums", name="row_sums"
+                )
+            row_sums = live["row_sums", i // NH]
             e = unit_pool.tile([P, T], BF16, tag="e")
             for b in range(T_BANKS):
                 nc.scalar.activation(
                     out=e[:, b * BANK : (b + 1) * BANK],
-                    in_=banks[b][:],
+                    in_=live["sc", i, b][:],
                     func=ACT.Exp,
-                    bias=shift[:],
+                    bias=live["shift", i][:],
                     scale=SCALE,
                     accum_out=row_sums[:, h * T_BANKS + b : h * T_BANKS + b + 1],
                 )
-            return e
+            live["e", i] = e
 
-        def pack(e):
-            words = e[:].bitcast(F32)
+        def flip_e(i):
+            words = live["e", i][:].bitcast(F32)
             flipped = psum_tr.tile([P, T_PASSES * 2, P], F32, tag="tr")
             for j in range(T_PASSES * 2):
                 nc.tensor.transpose(flipped[:, j, :], words[:, j * P : (j + 1) * P], ident_f32[:])
@@ -216,66 +243,85 @@ def tile_multiheadtokenattention_pa_t_kernel(tc, q, k, v, mask, Wo, bo, gamma, b
                 out=grouped[:].bitcast(F32).rearrange("p (c r u) -> p c r u", c=T_PASSES, u=2),
                 in_=flipped[:].rearrange("p (c u) r -> p c r u", u=2),
             )
+            live["e_grouped", i] = grouped
+
+        def quantise_e(i):
             codes = packed_pool.tile([P, T_PASSES * P], U32, tag="e_codes", align_bytes=64)
             scales = packed_pool.tile([P, T_PASSES * P], U8, tag="e_scales", align_bytes=64)
-            nc.vector.quantize_mx(out=codes[:].bitcast(FP8X4), scales=scales[:], in_=grouped[:])
-            return codes, scales
+            nc.vector.quantize_mx(
+                out=codes[:].bitcast(FP8X4), scales=scales[:], in_=live["e_grouped", i][:]
+            )
+            live["e_codes", i] = codes
+            live["e_scales", i] = scales
 
-        def finish_block(s, qt, packed, row_sums, v_codes, v_scales):
-            ctx_ps = psum_ctx.tile([P, HID], F32, tag="ctx")
-            for h in range(NH):
-                e_codes, e_scales = packed[h]
-                for c in range(T_PASSES):
-                    nc.tensor.matmul_mx(
-                        out=ctx_ps[:, h * DH : (h + 1) * DH],
-                        lhsT=e_codes[:, c * P : (c + 1) * P].bitcast(FP8X4),
-                        lhsT_scale=e_scales[:, c * P : (c + 1) * P],
-                        rhs=v_codes[:, c, h * DH : (h + 1) * DH].bitcast(FP8X4),
-                        rhs_scale=v_scales[:, c, h * DH : (h + 1) * DH],
-                        start=(c == 0),
-                        stop=(c == T_PASSES - 1),
-                    )
+        def invert_sums(n):
             total = small.tile([P, NH], F32, tag="total")
             nc.vector.tensor_reduce(
                 out=total[:],
-                in_=row_sums[:].rearrange("p (h b) -> p h b", b=T_BANKS),
+                in_=live["row_sums", n][:].rearrange("p (h b) -> p h b", b=T_BANKS),
                 axis=AX.X,
                 op=ALU.add,
             )
             inverse = small.tile([P, NH], F32, tag="inverse")
             nc.vector.reciprocal(out=inverse[:], in_=total[:])
+            live["inverse", n] = inverse
+
+        def attend(n):
+            s = units[n * NH][0]
+            v_codes, v_scales = v_of[s][1], v_of[s][2]
+            ctx_ps = psum_ctx.tile([P, HID], F32, tag="ctx")
+            for h in range(NH):
+                for c in range(T_PASSES):
+                    nc.tensor.matmul_mx(
+                        out=ctx_ps[:, h * DH : (h + 1) * DH],
+                        lhsT=live["e_codes", n * NH + h][:, c * P : (c + 1) * P].bitcast(FP8X4),
+                        lhsT_scale=live["e_scales", n * NH + h][:, c * P : (c + 1) * P],
+                        rhs=v_codes[:, c, h * DH : (h + 1) * DH].bitcast(FP8X4),
+                        rhs_scale=v_scales[:, c, h * DH : (h + 1) * DH],
+                        start=(c == 0),
+                        stop=(c == T_PASSES - 1),
+                    )
             res = block_pool.tile([P, HID], BF16, tag="res")
             nc.vector.tensor_tensor(
                 out=res[:].rearrange("p (h d) -> p h d", h=NH),
                 in0=ctx_ps[:].rearrange("p (h d) -> p h d", h=NH),
-                in1=inverse[:].unsqueeze(2).to_broadcast([P, NH, DH]),
+                in1=live["inverse", n][:].unsqueeze(2).to_broadcast([P, NH, DH]),
                 op=ALU.mult,
             )
+            live["res", n] = res
 
-            res_words = res[:].bitcast(F32)
+        def flip_res(n):
+            words = live["res", n][:].bitcast(F32)
             flipped = psum_tr.tile([P, 2, P], F32, tag="tr")
             for u in range(2):
-                nc.tensor.transpose(flipped[:, u, :], res_words[:, u * P : (u + 1) * P], ident_f32[:])
+                nc.tensor.transpose(flipped[:, u, :], words[:, u * P : (u + 1) * P], ident_f32[:])
             grouped = block_pool.tile([P, P * PACK], BF16, tag="res_grouped", align_bytes=64)
             nc.scalar.copy(
                 out=grouped[:].bitcast(F32).rearrange("p (r u) -> p r u", u=2),
                 in_=flipped[:].rearrange("p u r -> p r u"),
             )
-            res_codes = block_pool.tile([P, P], U32, tag="res_codes", align_bytes=64)
-            res_scales = block_pool.tile([P, P], U8, tag="res_scales", align_bytes=64)
-            nc.vector.quantize_mx(out=res_codes[:].bitcast(FP8X4), scales=res_scales[:], in_=grouped[:])
+            live["res_grouped", n] = grouped
 
+        def quantise_res(n):
+            codes = block_pool.tile([P, P], U32, tag="res_codes", align_bytes=64)
+            scales = block_pool.tile([P, P], U8, tag="res_scales", align_bytes=64)
+            nc.vector.quantize_mx(
+                out=codes[:].bitcast(FP8X4), scales=scales[:], in_=live["res_grouped", n][:]
+            )
+            live["res_codes", n] = codes
+            live["res_scales", n] = scales
+
+        def project(n):
             y_ps = psum_y.tile([P, HID], F32, tag="y")
             nc.tensor.matmul_mx(
                 out=y_ps[:],
-                lhsT=res_codes[:].bitcast(FP8X4),
-                lhsT_scale=res_scales[:],
+                lhsT=live["res_codes", n][:].bitcast(FP8X4),
+                lhsT_scale=live["res_scales", n][:],
                 rhs=wo_codes[:].bitcast(FP8X4),
                 rhs_scale=wo_scales[:],
                 start=True,
                 stop=True,
             )
-
             y = block_pool.tile([P, HID], F32, tag="y_sb")
             y_sum = small.tile([P, 1], F32, tag="y_sum")
             nc.vector.scalar_tensor_tensor(
@@ -283,14 +329,18 @@ def tile_multiheadtokenattention_pa_t_kernel(tc, q, k, v, mask, Wo, bo, gamma, b
                 accum_out=y_sum[:],
             )
             neg_mean = small.tile([P, 1], F32, tag="neg_mean")
-            nc.vector.tensor_scalar(
-                out=neg_mean[:], in0=y_sum[:], scalar1=-1.0 / HID, scalar2=None, op0=ALU.mult
+            nc.gpsimd.tensor_scalar(
+                out=neg_mean[:], in0=y_sum[:], scalar1=-1.0 / HID, scalar2=0.0, op0=ALU.mult, op1=ALU.add
             )
+            live["y", n] = y
+            live["neg_mean", n] = neg_mean
+
+        def deviation(n):
             squares = block_pool.tile([P, HID], BF16, tag="squares")
             dev2 = small.tile([P, 1], F32, tag="dev2")
             nc.scalar.activation(
-                out=squares[:], in_=y[:], func=ACT.Square, bias=neg_mean[:], scale=1.0,
-                accum_out=dev2[:],
+                out=squares[:], in_=live["y", n][:], func=ACT.Square, bias=live["neg_mean", n][:],
+                scale=1.0, accum_out=dev2[:],
             )
             var_eps = small.tile([P, 1], F32, tag="var_eps")
             nc.gpsimd.tensor_scalar(
@@ -298,42 +348,53 @@ def tile_multiheadtokenattention_pa_t_kernel(tc, q, k, v, mask, Wo, bo, gamma, b
             )
             rstd = small.tile([P, 1], F32, tag="rstd")
             nc.gpsimd.tensor_tensor(out=rstd[:], in0=var_eps[:], in1=minus_half[:], op=ALU.pow)
+            live["rstd", n] = rstd
+
+        def centre(n):
             centred = block_pool.tile([P, HID], F32, tag="centred")
             nc.vector.scalar_tensor_tensor(
-                out=centred[:], in0=y[:], scalar=neg_mean[:], in1=gamma_all[:], op0=ALU.add, op1=ALU.mult
+                out=centred[:], in0=live["y", n][:], scalar=live["neg_mean", n][:], in1=gamma_all[:],
+                op0=ALU.add, op1=ALU.mult,
             )
+            live["centred", n] = centred
+
+        def store(n):
+            s, qt, h = units[n * NH]
             result = block_pool.tile([P, HID], F32, tag="result")
             nc.vector.scalar_tensor_tensor(
-                out=result[:], in0=centred[:], scalar=rstd[:], in1=beta_all[:], op0=ALU.mult, op1=ALU.add
+                out=result[:], in0=live["centred", n][:], scalar=live["rstd", n][:], in1=beta_all[:],
+                op0=ALU.mult, op1=ALU.add,
             )
             nc.sync.dma_start(out=out[0, qt * P : (qt + 1) * P, s, :], in_=result[:])
 
-        units = [(s, qt, h) for s in range(S) for qt in range(Q_TILES) for h in range(NH)]
-        kT_of = {0: transpose_keys(0)}
-        transpose_queries(0)
-        v_of = {0: quantise_values(0)}
-        banks_of = {}
-        e_of = {}
-        sums_of = {}
-        packed_of = {}
-        for step in range(len(units) + 2):
-            if step < len(units):
+        block_stages = [invert_sums, attend, flip_res, quantise_res, project, deviation, centre, store]
+        BLOCK_LAG = 3
+        n_units = len(units)
+        per_sentence = Q_TILES * NH
+        for step in range(n_units + BLOCK_LAG + len(block_stages)):
+            if step < n_units:
+                scores(step)
+                bank_maxima(step)
+            if 0 <= step - 3 < n_units:
+                quantise_e(step - 3)
+            if step < n_units:
+                row_shift(step)
+            if 0 <= step - 1 < n_units:
+                exponentials(step - 1)
+            if 0 <= step - 2 < n_units:
+                flip_e(step - 2)
+            if step < n_units:
                 s, qt, h = units[step]
-                banks_of[step] = scores(s, qt, h, kT_of[s])
+                within = step - s * per_sentence
                 if s == 0 and h == 0 and qt + 1 < Q_TILES:
                     transpose_queries(qt + 1)
-                if qt == Q_TILES // 2 and h == 0 and s + 1 < S:
-                    kT_of[s + 1] = transpose_keys(s + 1)
-                    v_of[s + 1] = quantise_values(s + 1)
-            if 1 <= step <= len(units):
-                s, qt, h = units[step - 1]
-                if h == 0:
-                    sums_of[(s, qt)] = small.tile([P, NH * T_BANKS], F32, tag="row_sums", name="row_sums")
-                e_of[step - 1] = softmax(banks_of[step - 1], sums_of[(s, qt)], h)
-            if step >= 2:
-                s, qt, h = units[step - 2]
-                packed_of[h] = pack(e_of[step - 2])
-                if h == NH - 1:
-                    finish_block(
-                        s, qt, [packed_of[i] for i in range(NH)], sums_of[(s, qt)], v_of[s][0], v_of[s][1]
-                    )
+                if 1 <= within <= T_PASSES:
+                    group_values(s, within - 1)
+                if within == T_PASSES + 1:
+                    quantise_values(s)
+                if s + 1 < S and 0 <= within - per_sentence // 2 < T_TILES:
+                    transpose_keys(s + 1, within - per_sentence // 2)
+            for n, stage in enumerate(block_stages):
+                last_unit = step - BLOCK_LAG - n
+                if 0 <= last_unit < n_units and last_unit % NH == NH - 1:
+                    stage(last_unit // NH)

@@ -80,6 +80,8 @@ def tile_multiheadtokenattention_pa_t_kernel(tc, q, k, v, mask, Wo, bo, gamma, b
         make_identity(nc, ident_f32[:])
         minus_half = consts.tile([P, 1], F32)
         nc.vector.memset(minus_half[:], -0.5)
+        minus_one = consts.tile([P, NH], F32)
+        nc.vector.memset(minus_one[:], -1.0)
 
         mask_flipped = psum_tr.tile([P, P], BF16, tag="tr")
         nc.tensor.transpose(mask_flipped[:], mask_rows[:], ident_bf[:])
@@ -255,15 +257,11 @@ def tile_multiheadtokenattention_pa_t_kernel(tc, q, k, v, mask, Wo, bo, gamma, b
             live["e_scales", i] = scales
 
         def invert_sums(n):
+            by_bank = live["row_sums", n][:].rearrange("p (h b) -> p h b", b=T_BANKS)
             total = small.tile([P, NH], F32, tag="total")
-            nc.vector.tensor_reduce(
-                out=total[:],
-                in_=live["row_sums", n][:].rearrange("p (h b) -> p h b", b=T_BANKS),
-                axis=AX.X,
-                op=ALU.add,
-            )
+            nc.gpsimd.tensor_tensor(out=total[:], in0=by_bank[:, :, 0], in1=by_bank[:, :, 1], op=ALU.add)
             inverse = small.tile([P, NH], F32, tag="inverse")
-            nc.vector.reciprocal(out=inverse[:], in_=total[:])
+            nc.gpsimd.tensor_tensor(out=inverse[:], in0=total[:], in1=minus_one[:], op=ALU.pow)
             live["inverse", n] = inverse
 
         def attend(n):
@@ -282,12 +280,13 @@ def tile_multiheadtokenattention_pa_t_kernel(tc, q, k, v, mask, Wo, bo, gamma, b
                         stop=(c == T_PASSES - 1),
                     )
             res = block_pool.tile([P, HID], BF16, tag="res")
-            nc.vector.tensor_tensor(
-                out=res[:].rearrange("p (h d) -> p h d", h=NH),
-                in0=ctx_ps[:].rearrange("p (h d) -> p h d", h=NH),
-                in1=live["inverse", n][:].unsqueeze(2).to_broadcast([P, NH, DH]),
-                op=ALU.mult,
-            )
+            for h in range(NH):
+                nc.scalar.activation(
+                    out=res[:, h * DH : (h + 1) * DH],
+                    in_=ctx_ps[:, h * DH : (h + 1) * DH],
+                    func=ACT.Copy,
+                    scale=live["inverse", n][:, h : h + 1],
+                )
             live["res", n] = res
 
         def flip_res(n):

@@ -42,9 +42,8 @@ def tile_multiheadtokenattention_pa_t_kernel(tc, q, k, v, mask, Wo, bo, gamma, b
         block_pool = stack.enter_context(tc.tile_pool(name="block", bufs=2))
         small = stack.enter_context(tc.tile_pool(name="small", bufs=4))
         psum_sc = stack.enter_context(tc.psum_pool(name="psum_sc", bufs=2 * T_BANKS))
-        psum_tr = stack.enter_context(tc.psum_pool(name="psum_tr", bufs=2))
-        psum_ctx = stack.enter_context(tc.psum_pool(name="psum_ctx", bufs=1))
-        psum_y = stack.enter_context(tc.psum_pool(name="psum_y", bufs=1))
+        psum_tr = stack.enter_context(tc.psum_pool(name="psum_tr", bufs=3))
+        psum_mx = stack.enter_context(tc.psum_pool(name="psum_mx", bufs=1))
 
         mask_rows = consts.tile([P, P], BF16)
         nc.vector.memset(mask_rows[:], 0.0)
@@ -63,10 +62,14 @@ def tile_multiheadtokenattention_pa_t_kernel(tc, q, k, v, mask, Wo, bo, gamma, b
         bo_all = consts.tile([P, HID], BF16)
         gamma_all = consts.tile([P, HID], BF16)
         beta_all = consts.tile([P, HID], BF16)
-        nc.sync.dma_start(out=k_raw[0][:], in_=k_rows[0])
-        nc.sync.dma_start(out=q_raw[:], in_=q.rearrange("b (n p) f -> p (b n) f", p=P))
-        nc.sync.dma_start(out=wo_raw[:], in_=Wo.rearrange("(n p) f -> p n f", p=P))
+        q_rows = q.rearrange("b (n p) f -> p (b n) f", p=P)
+        half_tiles = T_TILES // T_BANKS
+        nc.sync.dma_start(out=q_raw[:, 0:1, :], in_=q_rows[:, 0:1, :])
+        nc.sync.dma_start(out=k_raw[0][:, 0:half_tiles, :], in_=k_rows[0][:, 0:half_tiles, :])
+        nc.sync.dma_start(out=k_raw[0][:, half_tiles:, :], in_=k_rows[0][:, half_tiles:, :])
+        nc.sync.dma_start(out=q_raw[:, 1:, :], in_=q_rows[:, 1:, :])
         nc.sync.dma_start(out=v_raw[0][:], in_=v_rows[0])
+        nc.sync.dma_start(out=wo_raw[:], in_=Wo.rearrange("(n p) f -> p n f", p=P))
         nc.sync.dma_start(out=bo_all[:], in_=bo.partition_broadcast(P))
         nc.sync.dma_start(out=gamma_all[:], in_=gamma.partition_broadcast(P))
         nc.sync.dma_start(out=beta_all[:], in_=beta.partition_broadcast(P))
@@ -94,9 +97,15 @@ def tile_multiheadtokenattention_pa_t_kernel(tc, q, k, v, mask, Wo, bo, gamma, b
             op0=ALU.mult,
         )
         mask_bias = consts.tile([P, S * T_TILES, P], F32)
-        nc.vector.tensor_copy(
-            out=mask_bias[:], in_=mask_col[:].unsqueeze(2).to_broadcast([P, S * T_TILES, P])
-        )
+
+        def spread_mask(s):
+            tiles = slice(s * T_TILES, (s + 1) * T_TILES)
+            nc.vector.tensor_copy(
+                out=mask_bias[:, tiles, :],
+                in_=mask_col[:, tiles].unsqueeze(2).to_broadcast([P, T_TILES, P]),
+            )
+
+        spread_mask(0)
 
         qT = consts.tile([P, NH, Q], BF16)
         kT_of = {}
@@ -110,15 +119,20 @@ def tile_multiheadtokenattention_pa_t_kernel(tc, q, k, v, mask, Wo, bo, gamma, b
                 )
             nc.vector.tensor_copy(out=qT[:, :, qt * P : (qt + 1) * P], in_=flipped[:])
 
-        def transpose_keys(s, tt):
-            if tt == 0:
+        def transpose_keys(s, h, b):
+            if h == 0 and b == 0:
                 kT_of[s] = sentence.tile([P, NH, T], BF16, tag="kT", name="kT")
-            flipped = psum_tr.tile([P, NH, P], BF16, tag="tr")
-            for h in range(NH):
+            flipped = psum_tr.tile([P, half_tiles, P], BF16, tag="tr")
+            for j in range(half_tiles):
                 nc.tensor.transpose(
-                    flipped[:, h, :], k_raw[s][:, tt, h * DH : (h + 1) * DH], ident_bf[:]
+                    flipped[:, j, :],
+                    k_raw[s][:, b * half_tiles + j, h * DH : (h + 1) * DH],
+                    ident_bf[:],
                 )
-            nc.scalar.copy(out=kT_of[s][:, :, tt * P : (tt + 1) * P], in_=flipped[:])
+            nc.scalar.copy(
+                out=kT_of[s][:, h, b * BANK : (b + 1) * BANK],
+                in_=flipped[:].rearrange("p j t -> p (j t)"),
+            )
 
         def group_values(s, c):
             if c == 0:
@@ -140,35 +154,39 @@ def tile_multiheadtokenattention_pa_t_kernel(tc, q, k, v, mask, Wo, bo, gamma, b
                 in_=grouped[:].rearrange("p c f j -> p (c f j)"),
             )
 
-        for tt in range(T_TILES):
-            transpose_keys(0, tt)
-        transpose_queries(0)
-
-        wo_words = wo_raw[:].bitcast(F32)
         wo_grouped = consts.tile([P, HID, PACK], BF16, align_bytes=64)
-        wo_grouped_words = wo_grouped[:].bitcast(F32)
-        for half in range(O_TILES // 2):
-            flipped = psum_tr.tile([P, 2, 2, P], F32, tag="tr")
-            for a in range(2):
-                for u in range(2):
-                    nc.tensor.transpose(
-                        flipped[:, a, u, :],
-                        wo_words[:, 2 * half + a, u * P : (u + 1) * P],
-                        ident_f32[:],
-                    )
-            nc.vector.tensor_copy(
-                out=wo_grouped_words[:, 2 * half * P : (2 * half + 2) * P, :].rearrange(
-                    "p (a o) u -> p a o u", a=2
-                ),
-                in_=flipped[:].rearrange("p a u o -> p a o u"),
-            )
         wo_codes = consts.tile([P, HID], U32, align_bytes=64)
         wo_scales = consts.tile([P, HID], U8, align_bytes=64)
-        nc.vector.quantize_mx(
-            out=wo_codes[:].bitcast(FP8X4),
-            scales=wo_scales[:],
-            in_=wo_grouped[:].rearrange("p o j -> p (o j)"),
-        )
+
+        def quantise_wo():
+            wo_words = wo_raw[:].bitcast(F32)
+            wo_grouped_words = wo_grouped[:].bitcast(F32)
+            for half in range(O_TILES // 2):
+                flipped = psum_tr.tile([P, 2, 2, P], F32, tag="tr")
+                for a in range(2):
+                    for u in range(2):
+                        nc.tensor.transpose(
+                            flipped[:, a, u, :],
+                            wo_words[:, 2 * half + a, u * P : (u + 1) * P],
+                            ident_f32[:],
+                        )
+                nc.vector.tensor_copy(
+                    out=wo_grouped_words[:, 2 * half * P : (2 * half + 2) * P, :].rearrange(
+                        "p (a o) u -> p a o u", a=2
+                    ),
+                    in_=flipped[:].rearrange("p a u o -> p a o u"),
+                )
+            nc.vector.quantize_mx(
+                out=wo_codes[:].bitcast(FP8X4),
+                scales=wo_scales[:],
+                in_=wo_grouped[:].rearrange("p o j -> p (o j)"),
+            )
+
+        transpose_queries(0)
+        for b in range(T_BANKS):
+            transpose_keys(0, 0, b)
+        for s in range(1, S):
+            spread_mask(s)
 
         units = [(s, qt, h) for s in range(S) for qt in range(Q_TILES) for h in range(NH)]
         live = {}
@@ -267,7 +285,7 @@ def tile_multiheadtokenattention_pa_t_kernel(tc, q, k, v, mask, Wo, bo, gamma, b
         def attend(n):
             s = units[n * NH][0]
             v_codes, v_scales = v_of[s][1], v_of[s][2]
-            ctx_ps = psum_ctx.tile([P, HID], F32, tag="ctx")
+            ctx_ps = psum_mx.tile([P, HID], F32, tag="mx")
             for h in range(NH):
                 for c in range(T_PASSES):
                     nc.tensor.matmul_mx(
@@ -280,13 +298,12 @@ def tile_multiheadtokenattention_pa_t_kernel(tc, q, k, v, mask, Wo, bo, gamma, b
                         stop=(c == T_PASSES - 1),
                     )
             res = block_pool.tile([P, HID], BF16, tag="res")
-            for h in range(NH):
-                nc.scalar.activation(
-                    out=res[:, h * DH : (h + 1) * DH],
-                    in_=ctx_ps[:, h * DH : (h + 1) * DH],
-                    func=ACT.Copy,
-                    scale=live["inverse", n][:, h : h + 1],
-                )
+            nc.vector.tensor_tensor(
+                out=res[:].rearrange("p (h d) -> p h d", h=NH),
+                in0=ctx_ps[:].rearrange("p (h d) -> p h d", h=NH),
+                in1=live["inverse", n][:].unsqueeze(2).to_broadcast([P, NH, DH]),
+                op=ALU.mult,
+            )
             live["res", n] = res
 
         def flip_res(n):
@@ -311,7 +328,7 @@ def tile_multiheadtokenattention_pa_t_kernel(tc, q, k, v, mask, Wo, bo, gamma, b
             live["res_scales", n] = scales
 
         def project(n):
-            y_ps = psum_y.tile([P, HID], F32, tag="y")
+            y_ps = psum_mx.tile([P, HID], F32, tag="mx")
             nc.tensor.matmul_mx(
                 out=y_ps[:],
                 lhsT=live["res_codes", n][:].bitcast(FP8X4),
@@ -385,14 +402,20 @@ def tile_multiheadtokenattention_pa_t_kernel(tc, q, k, v, mask, Wo, bo, gamma, b
             if step < n_units:
                 s, qt, h = units[step]
                 within = step - s * per_sentence
+                ahead = within - per_sentence // 2
+                if s == 0 and within + 1 < NH:
+                    for b in range(T_BANKS):
+                        transpose_keys(0, within + 1, b)
+                if s == 0 and within == NH:
+                    quantise_wo()
                 if s == 0 and h == 0 and qt + 1 < Q_TILES:
                     transpose_queries(qt + 1)
                 if 1 <= within <= T_PASSES:
                     group_values(s, within - 1)
                 if within == T_PASSES + 1:
                     quantise_values(s)
-                if s + 1 < S and 0 <= within - per_sentence // 2 < T_TILES:
-                    transpose_keys(s + 1, within - per_sentence // 2)
+                if s + 1 < S and 0 <= ahead < NH * T_BANKS:
+                    transpose_keys(s + 1, ahead // T_BANKS, ahead % T_BANKS)
             for n, stage in enumerate(block_stages):
                 last_unit = step - BLOCK_LAG - n
                 if 0 <= last_unit < n_units and last_unit % NH == NH - 1:

@@ -83,8 +83,6 @@ def tile_multiheadtokenattention_pa_t_kernel(tc, q, k, v, mask, Wo, bo, gamma, b
         make_identity(nc, ident_f32[:])
         minus_half = consts.tile([P, 1], F32)
         nc.vector.memset(minus_half[:], -0.5)
-        minus_one = consts.tile([P, NH], F32)
-        nc.vector.memset(minus_one[:], -1.0)
 
         mask_flipped = psum_tr.tile([P, P], BF16, tag="tr")
         nc.tensor.transpose(mask_flipped[:], mask_rows[:], ident_bf[:])
@@ -277,9 +275,12 @@ def tile_multiheadtokenattention_pa_t_kernel(tc, q, k, v, mask, Wo, bo, gamma, b
         def invert_sums(n):
             by_bank = live["row_sums", n][:].rearrange("p (h b) -> p h b", b=T_BANKS)
             total = small.tile([P, NH], F32, tag="total")
-            nc.gpsimd.tensor_tensor(out=total[:], in0=by_bank[:, :, 0], in1=by_bank[:, :, 1], op=ALU.add)
+            nc.vector.tensor_tensor(out=total[:], in0=by_bank[:, :, 0], in1=by_bank[:, :, 1], op=ALU.add)
+            live["total", n] = total
+
+        def finish_inverse(n):
             inverse = small.tile([P, NH], F32, tag="inverse")
-            nc.gpsimd.tensor_tensor(out=inverse[:], in0=total[:], in1=minus_one[:], op=ALU.pow)
+            nc.vector.reciprocal(out=inverse[:], in_=live["total", n][:])
             live["inverse", n] = inverse
 
         def attend(n):
@@ -383,18 +384,23 @@ def tile_multiheadtokenattention_pa_t_kernel(tc, q, k, v, mask, Wo, bo, gamma, b
             )
             nc.sync.dma_start(out=out[0, qt * P : (qt + 1) * P, s, :], in_=result[:])
 
-        block_stages = [invert_sums, attend, flip_res, quantise_res, project, deviation, centre, store]
+        block_stages = [attend, flip_res, quantise_res, project, deviation, centre, store]
         BLOCK_LAG = 3
         n_units = len(units)
         per_sentence = Q_TILES * NH
-        for step in range(n_units + BLOCK_LAG + len(block_stages)):
+        for step in range(n_units + BLOCK_LAG + 1 + len(block_stages)):
             if step < n_units:
                 scores(step)
                 bank_maxima(step)
+            ends_block = 0 <= step - BLOCK_LAG < n_units and (step - BLOCK_LAG) % NH == NH - 1
+            if ends_block:
+                invert_sums((step - BLOCK_LAG) // NH)
             if 0 <= step - 3 < n_units:
                 quantise_e(step - 3)
             if step < n_units:
                 row_shift(step)
+            if ends_block:
+                finish_inverse((step - BLOCK_LAG) // NH)
             if 0 <= step - 1 < n_units:
                 exponentials(step - 1)
             if 0 <= step - 2 < n_units:
@@ -417,6 +423,6 @@ def tile_multiheadtokenattention_pa_t_kernel(tc, q, k, v, mask, Wo, bo, gamma, b
                 if s + 1 < S and 0 <= ahead < NH * T_BANKS:
                     transpose_keys(s + 1, ahead // T_BANKS, ahead % T_BANKS)
             for n, stage in enumerate(block_stages):
-                last_unit = step - BLOCK_LAG - n
+                last_unit = step - BLOCK_LAG - 1 - n
                 if 0 <= last_unit < n_units and last_unit % NH == NH - 1:
                     stage(last_unit // NH)

@@ -24,6 +24,7 @@ T_TILES = T // P
 T_BANKS = T // BANK
 T_PASSES = T // K_PASS
 O_TILES = HID // P
+V_PARTS = 4
 SCALE = 1.0 / math.sqrt(DH)
 NEG = -10000.0
 EPS = 1e-12
@@ -132,24 +133,48 @@ def tile_multiheadtokenattention_pa_t_kernel(tc, q, k, v, mask, Wo, bo, gamma, b
                 in_=flipped[:].rearrange("p j t -> p (j t)"),
             )
 
+        def new_values(s):
+            v_of[s] = (
+                sentence.tile([P, T_PASSES, HID, PACK], BF16, tag="v_grouped", name="v_grouped", align_bytes=64),
+                sentence.tile([P, T_PASSES, HID], U32, tag="v_codes", name="v_codes", align_bytes=64),
+                sentence.tile([P, T_PASSES, HID], U8, tag="v_scales", name="v_scales", align_bytes=64),
+            )
+
         def group_values(s, c):
             if c == 0:
-                v_of[s] = (
-                    sentence.tile([P, T_PASSES, HID, PACK], BF16, tag="v_grouped", name="v_grouped", align_bytes=64),
-                    sentence.tile([P, T_PASSES, HID], U32, tag="v_codes", name="v_codes", align_bytes=64),
-                    sentence.tile([P, T_PASSES, HID], U8, tag="v_scales", name="v_scales", align_bytes=64),
-                )
+                new_values(s)
             nc.vector.tensor_copy(
                 out=v_of[s][0][:, c].rearrange("p f (u e) -> p f u e", e=2),
                 in_=v_raw[s][:, 2 * c : 2 * c + 2, :].rearrange("p u (e f) -> p f u e", e=2),
             )
 
-        def quantise_values(s):
+        def group_values_ahead(s, block):
+            if block == 0:
+                new_values(s)
+            opened = small.tile([P, 1], F32, tag="opened")
+            nc.gpsimd.tensor_scalar(
+                out=opened[:], in0=live["shift", step][:], scalar1=1.0, scalar2=0.0, op0=ALU.mult, op1=ALU.add
+            )
+            c, eighth = divmod(block, Q_TILES // T_PASSES)
+            width = HID * T_PASSES // Q_TILES
+            cols = slice(eighth * width, (eighth + 1) * width)
+            nc.gpsimd.tensor_scalar(
+                out=v_of[s][0][:, c, cols].rearrange("p f (u e) -> p f u e", e=2),
+                in0=v_raw[s][:, 2 * c : 2 * c + 2, :].rearrange("p u (e f) -> p f u e", e=2)[:, cols],
+                scalar1=1.0,
+                scalar2=0.0,
+                op0=ALU.mult,
+                op1=ALU.add,
+            )
+
+        def quantise_values(s, part):
             grouped, codes, scales = v_of[s]
+            c, half = divmod(part, 2)
+            cols = slice(half * HID // 2, (half + 1) * HID // 2)
             nc.vector.quantize_mx(
-                out=codes[:].rearrange("p c f -> p (c f)").bitcast(FP8X4),
-                scales=scales[:].rearrange("p c f -> p (c f)"),
-                in_=grouped[:].rearrange("p c f j -> p (c f j)"),
+                out=codes[:, c, cols].bitcast(FP8X4),
+                scales=scales[:, c, cols],
+                in_=grouped[:, c, cols].rearrange("p f j -> p (f j)"),
             )
 
         wo_grouped = consts.tile([P, HID, PACK], BF16, align_bytes=64)
@@ -359,9 +384,12 @@ def tile_multiheadtokenattention_pa_t_kernel(tc, q, k, v, mask, Wo, bo, gamma, b
                 out=squares[:], in_=live["y", n][:], func=ACT.Square, bias=live["neg_mean", n][:],
                 scale=1.0, accum_out=dev2[:],
             )
+            live["dev2", n] = dev2
+
+        def inverse_root(n):
             var_eps = small.tile([P, 1], F32, tag="var_eps")
-            nc.gpsimd.tensor_scalar(
-                out=var_eps[:], in0=dev2[:], scalar1=1.0 / HID, scalar2=EPS, op0=ALU.mult, op1=ALU.add
+            nc.vector.tensor_scalar(
+                out=var_eps[:], in0=live["dev2", n][:], scalar1=1.0 / HID, scalar2=EPS, op0=ALU.mult, op1=ALU.add
             )
             rstd = small.tile([P, 1], F32, tag="rstd")
             nc.gpsimd.tensor_tensor(out=rstd[:], in0=var_eps[:], in1=minus_half[:], op=ALU.pow)
@@ -374,6 +402,7 @@ def tile_multiheadtokenattention_pa_t_kernel(tc, q, k, v, mask, Wo, bo, gamma, b
                 op0=ALU.add, op1=ALU.mult,
             )
             live["centred", n] = centred
+            inverse_root(n)
 
         def store(n):
             s, qt, h = units[n * NH]
@@ -416,10 +445,12 @@ def tile_multiheadtokenattention_pa_t_kernel(tc, q, k, v, mask, Wo, bo, gamma, b
                     quantise_wo()
                 if s == 0 and h == 0 and qt + 1 < Q_TILES:
                     transpose_queries(qt + 1)
-                if 1 <= within <= T_PASSES:
+                if s == 0 and 1 <= within <= T_PASSES:
                     group_values(s, within - 1)
-                if within == T_PASSES + 1:
-                    quantise_values(s)
+                if 2 <= within < 2 + V_PARTS:
+                    quantise_values(s, within - 2)
+                if s + 1 < S and h == NH - 1:
+                    group_values_ahead(s + 1, qt)
                 if s + 1 < S and 0 <= ahead < NH * T_BANKS:
                     transpose_keys(s + 1, ahead // T_BANKS, ahead % T_BANKS)
             for n, stage in enumerate(block_stages):

@@ -40,11 +40,10 @@ def tile_multiheadtokenattention_pa_t_kernel(tc, q, k, v, mask, Wo, bo, gamma, b
         sentence = stack.enter_context(tc.tile_pool(name="sentence", bufs=2))
         unit_pool = stack.enter_context(tc.tile_pool(name="unit", bufs=3))
         packed_pool = stack.enter_context(tc.tile_pool(name="packed", bufs=2 * NH))
-        block_pool = stack.enter_context(tc.tile_pool(name="block", bufs=2))
-        small = stack.enter_context(tc.tile_pool(name="small", bufs=4))
-        psum_sc = stack.enter_context(tc.psum_pool(name="psum_sc", bufs=2 * T_BANKS))
+        block_pool = stack.enter_context(tc.tile_pool(name="block", bufs=3))
+        small = stack.enter_context(tc.tile_pool(name="small", bufs=6))
+        psum_sc = stack.enter_context(tc.psum_pool(name="psum_sc", bufs=5))
         psum_tr = stack.enter_context(tc.psum_pool(name="psum_tr", bufs=3))
-        psum_mx = stack.enter_context(tc.psum_pool(name="psum_mx", bufs=1))
 
         mask_rows = consts.tile([P, P], BF16)
         nc.vector.memset(mask_rows[:], 0.0)
@@ -151,20 +150,12 @@ def tile_multiheadtokenattention_pa_t_kernel(tc, q, k, v, mask, Wo, bo, gamma, b
         def group_values_ahead(s, block):
             if block == 0:
                 new_values(s)
-            opened = small.tile([P, 1], F32, tag="opened")
-            nc.gpsimd.tensor_scalar(
-                out=opened[:], in0=live["shift", step][:], scalar1=1.0, scalar2=0.0, op0=ALU.mult, op1=ALU.add
-            )
             c, eighth = divmod(block, Q_TILES // T_PASSES)
             width = HID * T_PASSES // Q_TILES
             cols = slice(eighth * width, (eighth + 1) * width)
-            nc.gpsimd.tensor_scalar(
+            nc.vector.tensor_copy(
                 out=v_of[s][0][:, c, cols].rearrange("p f (u e) -> p f u e", e=2),
-                in0=v_raw[s][:, 2 * c : 2 * c + 2, :].rearrange("p u (e f) -> p f u e", e=2)[:, cols],
-                scalar1=1.0,
-                scalar2=0.0,
-                op0=ALU.mult,
-                op1=ALU.add,
+                in_=v_raw[s][:, 2 * c : 2 * c + 2, :].rearrange("p u (e f) -> p f u e", e=2)[:, cols],
             )
 
         def quantise_values(s, part):
@@ -311,7 +302,7 @@ def tile_multiheadtokenattention_pa_t_kernel(tc, q, k, v, mask, Wo, bo, gamma, b
         def attend(n):
             s = units[n * NH][0]
             v_codes, v_scales = v_of[s][1], v_of[s][2]
-            ctx_ps = psum_mx.tile([P, HID], F32, tag="mx")
+            ctx_ps = psum_tr.tile([P, HID], F32, tag="tr")
             for h in range(NH):
                 for c in range(T_PASSES):
                     nc.tensor.matmul_mx(
@@ -354,7 +345,7 @@ def tile_multiheadtokenattention_pa_t_kernel(tc, q, k, v, mask, Wo, bo, gamma, b
             live["res_scales", n] = scales
 
         def project(n):
-            y_ps = psum_mx.tile([P, HID], F32, tag="mx")
+            y_ps = psum_tr.tile([P, HID], F32, tag="tr")
             nc.tensor.matmul_mx(
                 out=y_ps[:],
                 lhsT=live["res_codes", n][:].bitcast(FP8X4),
@@ -370,90 +361,171 @@ def tile_multiheadtokenattention_pa_t_kernel(tc, q, k, v, mask, Wo, bo, gamma, b
                 out=y[:], in0=y_ps[:], scalar=1.0, in1=bo_all[:], op0=ALU.mult, op1=ALU.add,
                 accum_out=y_sum[:],
             )
-            neg_mean = small.tile([P, 1], F32, tag="neg_mean")
-            nc.gpsimd.tensor_scalar(
-                out=neg_mean[:], in0=y_sum[:], scalar1=-1.0 / HID, scalar2=0.0, op0=ALU.mult, op1=ALU.add
-            )
             live["y", n] = y
-            live["neg_mean", n] = neg_mean
+            live["y_sum", n] = y_sum
 
         def deviation(n):
             squares = block_pool.tile([P, HID], BF16, tag="squares")
             dev2 = small.tile([P, 1], F32, tag="dev2")
             nc.scalar.activation(
-                out=squares[:], in_=live["y", n][:], func=ACT.Square, bias=live["neg_mean", n][:],
-                scale=1.0, accum_out=dev2[:],
+                out=squares[:], in_=live["y", n][:], func=ACT.Square, bias=live["y_sum", n][:],
+                scale=-1.0 * HID, accum_out=dev2[:],
             )
             live["dev2", n] = dev2
+
+        def minus_mean(n):
+            neg_mean = small.tile([P, 1], F32, tag="neg_mean")
+            nc.vector.tensor_scalar(
+                out=neg_mean[:], in0=live["y_sum", n][:], scalar1=-1.0 / HID, scalar2=None, op0=ALU.mult
+            )
+            live["neg_mean", n] = neg_mean
 
         def inverse_root(n):
             var_eps = small.tile([P, 1], F32, tag="var_eps")
             nc.vector.tensor_scalar(
-                out=var_eps[:], in0=live["dev2", n][:], scalar1=1.0 / HID, scalar2=EPS, op0=ALU.mult, op1=ALU.add
+                out=var_eps[:], in0=live["dev2", n][:], scalar1=1.0 / HID**3, scalar2=EPS, op0=ALU.mult, op1=ALU.add
             )
             rstd = small.tile([P, 1], F32, tag="rstd")
             nc.gpsimd.tensor_tensor(out=rstd[:], in0=var_eps[:], in1=minus_half[:], op=ALU.pow)
             live["rstd", n] = rstd
 
-        def centre(n):
-            centred = block_pool.tile([P, HID], F32, tag="centred")
+        def normalise(n):
+            normal = block_pool.tile([P, HID], F32, tag="normal")
+            nc.vector.tensor_scalar(
+                out=normal[:], in0=live["y", n][:], scalar1=live["neg_mean", n][:], scalar2=live["rstd", n][:],
+                op0=ALU.add, op1=ALU.mult,
+            )
+            live["normal", n] = normal
+            live["scaled", n] = block_pool.tile([P, HID], F32, tag="scaled", name="scaled")
+            live["result", n] = block_pool.tile([P, HID], F32, tag="result", name="result")
+
+        def times_gamma(n, cols):
+            nc.gpsimd.tensor_tensor(
+                out=live["scaled", n][:, cols], in0=live["normal", n][:, cols], in1=gamma_all[:, cols], op=ALU.mult
+            )
+
+        def plus_beta(n, cols):
+            nc.gpsimd.tensor_tensor(
+                out=live["result", n][:, cols], in0=live["scaled", n][:, cols], in1=beta_all[:, cols], op=ALU.add
+            )
+
+        def store(n):
+            s, qt, h = units[n * NH]
+            nc.sync.dma_start(out=out[0, qt * P : (qt + 1) * P, s, :], in_=live["result", n][:])
+
+        def gate(step):
+            opened = small.tile([P, 1], F32, tag="opened")
+            nc.gpsimd.tensor_scalar(
+                out=opened[:], in0=live["shift", step][:], scalar1=1.0, scalar2=0.0, op0=ALU.mult, op1=ALU.add
+            )
+
+        def centre_v(n):
+            centred = block_pool.tile([P, HID], F32, tag="scaled", name="centred")
             nc.vector.scalar_tensor_tensor(
                 out=centred[:], in0=live["y", n][:], scalar=live["neg_mean", n][:], in1=gamma_all[:],
                 op0=ALU.add, op1=ALU.mult,
             )
-            live["centred", n] = centred
-            inverse_root(n)
+            live["scaled", n] = centred
 
-        def store(n):
+        def finish_v(n, parts):
             s, qt, h = units[n * NH]
-            result = block_pool.tile([P, HID], F32, tag="result")
-            nc.vector.scalar_tensor_tensor(
-                out=result[:], in0=live["centred", n][:], scalar=live["rstd", n][:], in1=beta_all[:],
-                op0=ALU.mult, op1=ALU.add,
-            )
-            nc.sync.dma_start(out=out[0, qt * P : (qt + 1) * P, s, :], in_=result[:])
+            result = block_pool.tile([P, HID], F32, tag="result", name="result")
+            for i in range(parts):
+                cols = slice(i * HID // parts, (i + 1) * HID // parts)
+                nc.vector.scalar_tensor_tensor(
+                    out=result[:, cols], in0=live["scaled", n][:, cols], scalar=live["rstd", n][:], in1=beta_all[:, cols],
+                    op0=ALU.mult, op1=ALU.add,
+                )
+                nc.sync.dma_start(out=out[0, qt * P : (qt + 1) * P, s, cols], in_=result[:, cols])
 
-        block_stages = [attend, flip_res, quantise_res, project, deviation, centre, store]
-        BLOCK_LAG = 3
         n_units = len(units)
         per_sentence = Q_TILES * NH
-        for step in range(n_units + BLOCK_LAG + 1 + len(block_stages)):
-            if step < n_units:
-                scores(step)
-                bank_maxima(step)
-            ends_block = 0 <= step - BLOCK_LAG < n_units and (step - BLOCK_LAG) % NH == NH - 1
-            if ends_block:
-                invert_sums((step - BLOCK_LAG) // NH)
-            if 0 <= step - 3 < n_units:
+
+        def at(stage, lag):
+            last = step - lag
+            if 0 <= last < n_units and last % NH == NH - 1:
+                stage(last // NH)
+
+        for step in range(n_units):
+            s, qt, h = units[step]
+            within = step - s * per_sentence
+            scores(step)
+            bank_maxima(step)
+            at(finish_inverse, 4)
+            if step >= 3:
                 quantise_e(step - 3)
-            if step < n_units:
-                row_shift(step)
-            if ends_block:
-                finish_inverse((step - BLOCK_LAG) // NH)
-            if 0 <= step - 1 < n_units:
-                exponentials(step - 1)
-            if 0 <= step - 2 < n_units:
-                flip_e(step - 2)
-            if step < n_units:
-                s, qt, h = units[step]
-                within = step - s * per_sentence
-                ahead = within - per_sentence // 2
-                if s == 0 and within + 1 < NH:
-                    for b in range(T_BANKS):
-                        transpose_keys(0, within + 1, b)
-                if s == 0 and within == NH:
-                    quantise_wo()
-                if s == 0 and h == 0 and qt + 1 < Q_TILES:
-                    transpose_queries(qt + 1)
-                if s == 0 and 1 <= within <= T_PASSES:
-                    group_values(s, within - 1)
+            row_shift(step)
+            at(invert_sums, 3)
+            at(minus_mean, 8)
+            at(quantise_res, 6)
+            at(inverse_root, 9)
+            at(normalise, 10)
+            if h == 0 and step > 0:
+                s0, qt0, h0 = units[step - 1]
+                if s0 + 1 < S:
+                    group_values_ahead(s0 + 1, qt0)
+            if s == 0:
                 if 2 <= within < 2 + V_PARTS:
                     quantise_values(s, within - 2)
-                if s + 1 < S and h == NH - 1:
-                    group_values_ahead(s + 1, qt)
-                if s + 1 < S and 0 <= ahead < NH * T_BANKS:
-                    transpose_keys(s + 1, ahead // T_BANKS, ahead % T_BANKS)
-            for n, stage in enumerate(block_stages):
-                last_unit = step - BLOCK_LAG - 1 - n
-                if 0 <= last_unit < n_units and last_unit % NH == NH - 1:
-                    stage(last_unit // NH)
+            elif within in (0, 1, 4, 5):
+                quantise_values(s, (0, 1, 4, 5).index(within))
+            at(attend, 4)
+            at(project, 7)
+            at(lambda n: times_gamma(n, slice(0, 256)), 10)
+            at(lambda n: gate(step), 11)
+            at(lambda n: times_gamma(n, slice(256, 512)), 11)
+            at(lambda n: plus_beta(n, slice(0, 128)), 11)
+            at(lambda n: gate(step), 12)
+            at(lambda n: plus_beta(n, slice(128, 512)), 12)
+            at(store, 12)
+            if step >= 1:
+                exponentials(step - 1)
+            if step >= 2:
+                flip_e(step - 2)
+            ahead = within - per_sentence // 2
+            if s == 0 and within + 1 < NH:
+                for b in range(T_BANKS):
+                    transpose_keys(0, within + 1, b)
+            if s == 0 and within == NH:
+                quantise_wo()
+            if s == 0 and h == 0 and qt + 1 < Q_TILES:
+                transpose_queries(qt + 1)
+            if s == 0 and 1 <= within <= T_PASSES:
+                group_values(s, within - 1)
+            if s + 1 < S and 0 <= ahead < NH * T_BANKS:
+                transpose_keys(s + 1, ahead // T_BANKS, ahead % T_BANKS)
+            at(flip_res, 5)
+            if step < n_units - 1:
+                at(deviation, 8)
+
+        last = n_units - 1
+        end = n_units // NH - 1
+        exponentials(last)
+        quantise_e(last - 2)
+        invert_sums(end)
+        centre_v(end - 2)
+        flip_e(last - 1)
+        flip_e(last)
+        quantise_e(last - 1)
+        finish_inverse(end)
+        flip_res(end - 1)
+        quantise_e(last)
+        deviation(end - 2)
+        quantise_res(end - 1)
+        inverse_root(end - 2)
+        attend(end)
+        project(end - 1)
+        flip_res(end)
+        minus_mean(end - 1)
+        quantise_res(end)
+        deviation(end - 1)
+        finish_v(end - 2, 1)
+        inverse_root(end - 1)
+        project(end)
+        centre_v(end - 1)
+        minus_mean(end)
+        deviation(end)
+        finish_v(end - 1, 1)
+        inverse_root(end)
+        centre_v(end)
+        finish_v(end, 2)

@@ -67,15 +67,15 @@ def tile_multiheadtokenattention_pa_t_kernel(tc, q, k, v, mask, Wo, bo, gamma, b
         nc.sync.dma_start(out=q_raw[:, 0:1, :], in_=q_rows[:, 0:1, :])
         nc.sync.dma_start(out=k_raw[0][:, 0:half_tiles, :], in_=k_rows[0][:, 0:half_tiles, :])
         nc.sync.dma_start(out=k_raw[0][:, half_tiles:, :], in_=k_rows[0][:, half_tiles:, :])
-        nc.sync.dma_start(out=q_raw[:, 1:, :], in_=q_rows[:, 1:, :])
         nc.sync.dma_start(out=v_raw[0][:], in_=v_rows[0])
+        nc.sync.dma_start(out=q_raw[:, 1:, :], in_=q_rows[:, 1:, :])
         nc.sync.dma_start(out=wo_raw[:], in_=Wo.rearrange("(n p) f -> p n f", p=P))
         nc.sync.dma_start(out=bo_all[:], in_=bo.partition_broadcast(P))
         nc.sync.dma_start(out=gamma_all[:], in_=gamma.partition_broadcast(P))
         nc.sync.dma_start(out=beta_all[:], in_=beta.partition_broadcast(P))
         for s in range(1, S):
-            nc.sync.dma_start(out=k_raw[s][:], in_=k_rows[s])
             nc.sync.dma_start(out=v_raw[s][:], in_=v_rows[s])
+            nc.sync.dma_start(out=k_raw[s][:], in_=k_rows[s])
 
         ident_bf = consts.tile([P, P], BF16)
         make_identity(nc, ident_bf[:])
@@ -83,6 +83,14 @@ def tile_multiheadtokenattention_pa_t_kernel(tc, q, k, v, mask, Wo, bo, gamma, b
         make_identity(nc, ident_f32[:])
         minus_half = consts.tile([P, 1], F32)
         nc.vector.memset(minus_half[:], -0.5)
+        zeros = consts.tile([P, 2], F32)
+        nc.vector.memset(zeros[:], 0.0)
+        eps_row = consts.tile([P, 2], F32)
+        nc.vector.tensor_copy(out=eps_row[:, 0:1], in_=zeros[:, 0:1])
+        nc.vector.tensor_scalar(
+            out=eps_row[:, 1:2], in0=zeros[:, 1:2], scalar1=EPS * HID**2, scalar2=None, op0=ALU.add
+        )
+        gamma_hid = consts.tile([P, HID], BF16)
 
         mask_flipped = psum_tr.tile([P, P], BF16, tag="tr")
         nc.tensor.transpose(mask_flipped[:], mask_rows[:], ident_bf[:])
@@ -117,7 +125,7 @@ def tile_multiheadtokenattention_pa_t_kernel(tc, q, k, v, mask, Wo, bo, gamma, b
                 )
             nc.vector.tensor_copy(out=qT[:, :, qt * P : (qt + 1) * P], in_=flipped[:])
 
-        def transpose_keys(s, h, b):
+        def transpose_keys(s, h, b, copy=nc.scalar.copy):
             if h == 0 and b == 0:
                 kT_of[s] = sentence.tile([P, NH, T], BF16, tag="kT", name="kT")
             flipped = psum_tr.tile([P, half_tiles, P], BF16, tag="tr")
@@ -127,7 +135,7 @@ def tile_multiheadtokenattention_pa_t_kernel(tc, q, k, v, mask, Wo, bo, gamma, b
                     k_raw[s][:, b * half_tiles + j, h * DH : (h + 1) * DH],
                     ident_bf[:],
                 )
-            nc.scalar.copy(
+            copy(
                 out=kT_of[s][:, h, b * BANK : (b + 1) * BANK],
                 in_=flipped[:].rearrange("p j t -> p (j t)"),
             )
@@ -142,9 +150,10 @@ def tile_multiheadtokenattention_pa_t_kernel(tc, q, k, v, mask, Wo, bo, gamma, b
         def group_values(s, c):
             if c == 0:
                 new_values(s)
-            nc.vector.tensor_copy(
+            nc.gpsimd.tensor_scalar(
                 out=v_of[s][0][:, c].rearrange("p f (u e) -> p f u e", e=2),
-                in_=v_raw[s][:, 2 * c : 2 * c + 2, :].rearrange("p u (e f) -> p f u e", e=2),
+                in0=v_raw[s][:, 2 * c : 2 * c + 2, :].rearrange("p u (e f) -> p f u e", e=2),
+                scalar1=1.0, scalar2=0.0, op0=ALU.mult, op1=ALU.add,
             )
 
         def group_values_ahead(s, block):
@@ -153,9 +162,12 @@ def tile_multiheadtokenattention_pa_t_kernel(tc, q, k, v, mask, Wo, bo, gamma, b
             c, eighth = divmod(block, Q_TILES // T_PASSES)
             width = HID * T_PASSES // Q_TILES
             cols = slice(eighth * width, (eighth + 1) * width)
-            nc.vector.tensor_copy(
+            one = small.tile([P, 1], F32, tag="one")
+            nc.vector.memset(one[:], 1.0)
+            nc.gpsimd.tensor_scalar(
                 out=v_of[s][0][:, c, cols].rearrange("p f (u e) -> p f u e", e=2),
-                in_=v_raw[s][:, 2 * c : 2 * c + 2, :].rearrange("p u (e f) -> p f u e", e=2)[:, cols],
+                in0=v_raw[s][:, 2 * c : 2 * c + 2, :].rearrange("p u (e f) -> p f u e", e=2)[:, cols],
+                scalar1=one[:], scalar2=0.0, op0=ALU.mult, op1=ALU.add,
             )
 
         def quantise_values(s, part):
@@ -172,24 +184,25 @@ def tile_multiheadtokenattention_pa_t_kernel(tc, q, k, v, mask, Wo, bo, gamma, b
         wo_codes = consts.tile([P, HID], U32, align_bytes=64)
         wo_scales = consts.tile([P, HID], U8, align_bytes=64)
 
-        def quantise_wo():
+        def group_wo(half):
             wo_words = wo_raw[:].bitcast(F32)
             wo_grouped_words = wo_grouped[:].bitcast(F32)
-            for half in range(O_TILES // 2):
-                flipped = psum_tr.tile([P, 2, 2, P], F32, tag="tr")
-                for a in range(2):
-                    for u in range(2):
-                        nc.tensor.transpose(
-                            flipped[:, a, u, :],
-                            wo_words[:, 2 * half + a, u * P : (u + 1) * P],
-                            ident_f32[:],
-                        )
-                nc.vector.tensor_copy(
-                    out=wo_grouped_words[:, 2 * half * P : (2 * half + 2) * P, :].rearrange(
-                        "p (a o) u -> p a o u", a=2
-                    ),
-                    in_=flipped[:].rearrange("p a u o -> p a o u"),
-                )
+            flipped = psum_tr.tile([P, 2, 2, P], F32, tag="tr")
+            for a in range(2):
+                for u in range(2):
+                    nc.tensor.transpose(
+                        flipped[:, a, u, :],
+                        wo_words[:, 2 * half + a, u * P : (u + 1) * P],
+                        ident_f32[:],
+                    )
+            nc.scalar.copy(
+                out=wo_grouped_words[:, 2 * half * P : (2 * half + 2) * P, :].rearrange(
+                    "p (a o) u -> p a o u", a=2
+                ),
+                in_=flipped[:].rearrange("p a u o -> p a o u"),
+            )
+
+        def quantise_wo():
             nc.vector.quantize_mx(
                 out=wo_codes[:].bitcast(FP8X4),
                 scales=wo_scales[:],
@@ -197,8 +210,9 @@ def tile_multiheadtokenattention_pa_t_kernel(tc, q, k, v, mask, Wo, bo, gamma, b
             )
 
         transpose_queries(0)
-        for b in range(T_BANKS):
-            transpose_keys(0, 0, b)
+        transpose_keys(0, 0, 0)
+        transpose_keys(0, 1, 0, nc.vector.tensor_copy)
+        transpose_keys(0, 0, 1)
         for s in range(1, S):
             spread_mask(s)
 
@@ -267,17 +281,41 @@ def tile_multiheadtokenattention_pa_t_kernel(tc, q, k, v, mask, Wo, bo, gamma, b
                 )
             live["e", i] = e
 
-        def flip_e(i):
+        def flip_e(i, copy=nc.scalar.copy):
             words = live["e", i][:].bitcast(F32)
             flipped = psum_tr.tile([P, T_PASSES * 2, P], F32, tag="tr")
             for j in range(T_PASSES * 2):
                 nc.tensor.transpose(flipped[:, j, :], words[:, j * P : (j + 1) * P], ident_f32[:])
             grouped = unit_pool.tile([P, T_PASSES * P * PACK], BF16, tag="e_grouped", align_bytes=64)
-            nc.scalar.copy(
+            copy(
                 out=grouped[:].bitcast(F32).rearrange("p (c r u) -> p c r u", c=T_PASSES, u=2),
                 in_=flipped[:].rearrange("p (c u) r -> p c r u", u=2),
             )
             live["e_grouped", i] = grouped
+
+        def flip_last(i):
+            words = live["e", i][:].bitcast(F32)
+            grouped = unit_pool.tile([P, T_PASSES * P * PACK], BF16, tag="e_grouped", name="grouped", align_bytes=64)
+            for c in range(T_PASSES):
+                flipped = psum_tr.tile([P, 2, P], F32, tag="tr", name="flipped")
+                for u in range(2):
+                    nc.tensor.transpose(flipped[:, u, :], words[:, (2 * c + u) * P : (2 * c + u + 1) * P], ident_f32[:])
+                (nc.scalar.copy, nc.vector.tensor_copy)[c](
+                    out=grouped[:, c * P * PACK : (c + 1) * P * PACK].bitcast(F32).rearrange("p (r u) -> p r u", u=2),
+                    in_=flipped[:].rearrange("p u r -> p r u"),
+                )
+            live["e_grouped", i] = grouped
+
+        def quantise_last(i):
+            codes = packed_pool.tile([P, T_PASSES * P], U32, tag="e_codes", name="codes", align_bytes=64)
+            scales = packed_pool.tile([P, T_PASSES * P], U8, tag="e_scales", name="scales", align_bytes=64)
+            for c in range(T_PASSES):
+                nc.vector.quantize_mx(
+                    out=codes[:, c * P : (c + 1) * P].bitcast(FP8X4), scales=scales[:, c * P : (c + 1) * P],
+                    in_=live["e_grouped", i][:, c * P * PACK : (c + 1) * P * PACK],
+                )
+            live["e_codes", i] = codes
+            live["e_scales", i] = scales
 
         def quantise_e(i):
             codes = packed_pool.tile([P, T_PASSES * P], U32, tag="e_codes", align_bytes=64)
@@ -299,11 +337,13 @@ def tile_multiheadtokenattention_pa_t_kernel(tc, q, k, v, mask, Wo, bo, gamma, b
             nc.vector.reciprocal(out=inverse[:], in_=live["total", n][:])
             live["inverse", n] = inverse
 
-        def attend(n):
+        def attend(n, heads=range(NH)):
             s = units[n * NH][0]
             v_codes, v_scales = v_of[s][1], v_of[s][2]
             ctx_ps = psum_tr.tile([P, HID], F32, tag="tr")
-            for h in range(NH):
+            if heads[0] == 0:
+                live["res", n] = block_pool.tile([P, HID], BF16, tag="res", name="res")
+            for h in heads:
                 for c in range(T_PASSES):
                     nc.tensor.matmul_mx(
                         out=ctx_ps[:, h * DH : (h + 1) * DH],
@@ -314,14 +354,13 @@ def tile_multiheadtokenattention_pa_t_kernel(tc, q, k, v, mask, Wo, bo, gamma, b
                         start=(c == 0),
                         stop=(c == T_PASSES - 1),
                     )
-            res = block_pool.tile([P, HID], BF16, tag="res")
+            cols = slice(heads[0] * DH, (heads[-1] + 1) * DH)
             nc.vector.tensor_tensor(
-                out=res[:].rearrange("p (h d) -> p h d", h=NH),
-                in0=ctx_ps[:].rearrange("p (h d) -> p h d", h=NH),
-                in1=live["inverse", n][:].unsqueeze(2).to_broadcast([P, NH, DH]),
+                out=live["res", n][:, cols].rearrange("p (h d) -> p h d", d=DH),
+                in0=ctx_ps[:, cols].rearrange("p (h d) -> p h d", d=DH),
+                in1=live["inverse", n][:, heads[0] : heads[-1] + 1].unsqueeze(2).to_broadcast([P, len(heads), DH]),
                 op=ALU.mult,
             )
-            live["res", n] = res
 
         def flip_res(n):
             words = live["res", n][:].bitcast(F32)
@@ -356,52 +395,50 @@ def tile_multiheadtokenattention_pa_t_kernel(tc, q, k, v, mask, Wo, bo, gamma, b
                 stop=True,
             )
             y = block_pool.tile([P, HID], F32, tag="y_sb")
-            y_sum = small.tile([P, 1], F32, tag="y_sum")
+            stats = small.tile([P, 2], F32, tag="stats")
             nc.vector.scalar_tensor_tensor(
                 out=y[:], in0=y_ps[:], scalar=1.0, in1=bo_all[:], op0=ALU.mult, op1=ALU.add,
-                accum_out=y_sum[:],
+                accum_out=stats[:, 0:1],
             )
             live["y", n] = y
-            live["y_sum", n] = y_sum
+            live["stats", n] = stats
 
         def deviation(n):
+            stats = live["stats", n]
             squares = block_pool.tile([P, HID], BF16, tag="squares")
-            dev2 = small.tile([P, 1], F32, tag="dev2")
             nc.scalar.activation(
-                out=squares[:], in_=live["y", n][:], func=ACT.Square, bias=live["y_sum", n][:],
-                scale=-1.0 * HID, accum_out=dev2[:],
+                out=squares[:], in_=live["y", n][:], func=ACT.Square, bias=stats[:, 0:1],
+                scale=-1.0 * HID, accum_out=stats[:, 1:2],
             )
-            live["dev2", n] = dev2
 
-        def minus_mean(n):
-            neg_mean = small.tile([P, 1], F32, tag="neg_mean")
-            nc.vector.tensor_scalar(
-                out=neg_mean[:], in0=live["y_sum", n][:], scalar1=-1.0 / HID, scalar2=None, op0=ALU.mult
-            )
-            live["neg_mean", n] = neg_mean
-
-        def inverse_root(n):
-            var_eps = small.tile([P, 1], F32, tag="var_eps")
-            nc.vector.tensor_scalar(
-                out=var_eps[:], in0=live["dev2", n][:], scalar1=1.0 / HID**3, scalar2=EPS, op0=ALU.mult, op1=ALU.add
+        def moments(n):
+            both = small.tile([P, 2], F32, tag="moments")
+            nc.vector.scalar_tensor_tensor(
+                out=both[:], in0=live["stats", n][:], scalar=1.0 / HID, in1=eps_row[:], op0=ALU.mult, op1=ALU.add
             )
             rstd = small.tile([P, 1], F32, tag="rstd")
-            nc.gpsimd.tensor_tensor(out=rstd[:], in0=var_eps[:], in1=minus_half[:], op=ALU.pow)
+            nc.gpsimd.tensor_tensor(out=rstd[:], in0=both[:, 1:2], in1=minus_half[:], op=ALU.pow)
+            live["mean", n] = both
             live["rstd", n] = rstd
 
-        def normalise(n):
-            normal = block_pool.tile([P, HID], F32, tag="normal")
+        def normalise(n, cols):
+            if cols.start == 0:
+                live["normal", n] = block_pool.tile([P, HID], F32, tag="normal", name="normal")
+                live["scaled", n] = block_pool.tile([P, HID], F32, tag="scaled", name="scaled")
+                live["result", n] = block_pool.tile([P, HID], F32, tag="result", name="result")
             nc.vector.tensor_scalar(
-                out=normal[:], in0=live["y", n][:], scalar1=live["neg_mean", n][:], scalar2=live["rstd", n][:],
-                op0=ALU.add, op1=ALU.mult,
+                out=live["normal", n][:, cols], in0=live["y", n][:, cols], scalar1=live["mean", n][:, 0:1], scalar2=live["rstd", n][:],
+                op0=ALU.subtract, op1=ALU.mult,
             )
-            live["normal", n] = normal
-            live["scaled", n] = block_pool.tile([P, HID], F32, tag="scaled", name="scaled")
-            live["result", n] = block_pool.tile([P, HID], F32, tag="result", name="result")
 
         def times_gamma(n, cols):
             nc.gpsimd.tensor_tensor(
-                out=live["scaled", n][:, cols], in0=live["normal", n][:, cols], in1=gamma_all[:, cols], op=ALU.mult
+                out=live["scaled", n][:, cols], in0=live["normal", n][:, cols], in1=gamma_hid[:, cols], op=ALU.mult
+            )
+
+        def vector_gamma(n, cols):
+            nc.vector.tensor_tensor(
+                out=live["scaled", n][:, cols], in0=live["normal", n][:, cols], in1=gamma_hid[:, cols], op=ALU.mult
             )
 
         def plus_beta(n, cols):
@@ -413,17 +450,11 @@ def tile_multiheadtokenattention_pa_t_kernel(tc, q, k, v, mask, Wo, bo, gamma, b
             s, qt, h = units[n * NH]
             nc.sync.dma_start(out=out[0, qt * P : (qt + 1) * P, s, :], in_=live["result", n][:])
 
-        def gate(step):
-            opened = small.tile([P, 1], F32, tag="opened")
-            nc.gpsimd.tensor_scalar(
-                out=opened[:], in0=live["shift", step][:], scalar1=1.0, scalar2=0.0, op0=ALU.mult, op1=ALU.add
-            )
-
         def centre_v(n):
             centred = block_pool.tile([P, HID], F32, tag="scaled", name="centred")
             nc.vector.scalar_tensor_tensor(
-                out=centred[:], in0=live["y", n][:], scalar=live["neg_mean", n][:], in1=gamma_all[:],
-                op0=ALU.add, op1=ALU.mult,
+                out=centred[:], in0=live["y", n][:], scalar=live["mean", n][:, 0:1], in1=gamma_hid[:],
+                op0=ALU.subtract, op1=ALU.mult,
             )
             live["scaled", n] = centred
 
@@ -456,44 +487,46 @@ def tile_multiheadtokenattention_pa_t_kernel(tc, q, k, v, mask, Wo, bo, gamma, b
                 quantise_e(step - 3)
             row_shift(step)
             at(invert_sums, 3)
-            at(minus_mean, 8)
             at(quantise_res, 6)
-            at(inverse_root, 9)
-            at(normalise, 10)
-            if h == 0 and step > 0:
-                s0, qt0, h0 = units[step - 1]
-                if s0 + 1 < S:
-                    group_values_ahead(s0 + 1, qt0)
-            if s == 0:
-                if 2 <= within < 2 + V_PARTS:
-                    quantise_values(s, within - 2)
-            elif within in (0, 1, 4, 5):
-                quantise_values(s, (0, 1, 4, 5).index(within))
+            at(moments, 9)
+            at(lambda n: normalise(n, slice(0, 512)), 11)
+            at(lambda n: vector_gamma(n, slice(480, 512)), 12)
+            if s == 0 and 3 <= within < 3 + V_PARTS:
+                quantise_values(s, within - 3)
+            if s > 0 and h < 2 and qt < V_PARTS // 2:
+                quantise_values(s, 2 * qt + h)
+            if h == 1 and s + 1 < S:
+                group_values_ahead(s + 1, qt)
             at(attend, 4)
             at(project, 7)
-            at(lambda n: times_gamma(n, slice(0, 256)), 10)
-            at(lambda n: gate(step), 11)
-            at(lambda n: times_gamma(n, slice(256, 512)), 11)
-            at(lambda n: plus_beta(n, slice(0, 128)), 11)
-            at(lambda n: gate(step), 12)
-            at(lambda n: plus_beta(n, slice(128, 512)), 12)
+            at(lambda n: times_gamma(n, slice(0, 480)), 11)
+            at(lambda n: plus_beta(n, slice(0, 512)), 12)
             at(store, 12)
             if step >= 1:
                 exponentials(step - 1)
             if step >= 2:
-                flip_e(step - 2)
+                flip_e(step - 2, nc.vector.tensor_copy if step == n_units - 1 else nc.scalar.copy)
             ahead = within - per_sentence // 2
-            if s == 0 and within + 1 < NH:
+            if step == 0:
+                transpose_keys(0, 1, 1)
+            if s == 0 and within + 2 < NH:
                 for b in range(T_BANKS):
-                    transpose_keys(0, within + 1, b)
-            if s == 0 and within == NH:
+                    transpose_keys(0, within + 2, b)
+            if step == 4:
+                group_wo(0)
+            if step == 5:
+                group_wo(1)
+            if step == 6:
                 quantise_wo()
-            if s == 0 and h == 0 and qt + 1 < Q_TILES:
+            if s == 0 and h == 1 and qt + 1 < Q_TILES:
                 transpose_queries(qt + 1)
-            if s == 0 and 1 <= within <= T_PASSES:
-                group_values(s, within - 1)
+            if step == 0:
+                group_values(0, 0)
+                group_values(0, 1)
+            if step == 7:
+                nc.vector.tensor_scalar(out=gamma_hid[:], in0=gamma_all[:], scalar1=1.0 * HID, scalar2=None, op0=ALU.mult)
             if s + 1 < S and 0 <= ahead < NH * T_BANKS:
-                transpose_keys(s + 1, ahead // T_BANKS, ahead % T_BANKS)
+                transpose_keys(s + 1, ahead // T_BANKS, ahead % T_BANKS, nc.vector.tensor_copy if ahead % 2 == 1 else nc.scalar.copy)
             at(flip_res, 5)
             if step < n_units - 1:
                 at(deviation, 8)
@@ -501,31 +534,30 @@ def tile_multiheadtokenattention_pa_t_kernel(tc, q, k, v, mask, Wo, bo, gamma, b
         last = n_units - 1
         end = n_units // NH - 1
         exponentials(last)
-        quantise_e(last - 2)
+        flip_e(last - 1, nc.vector.tensor_copy)
+        flip_res(end - 1)
         invert_sums(end)
-        centre_v(end - 2)
-        flip_e(last - 1)
-        flip_e(last)
+        quantise_e(last - 2)
         quantise_e(last - 1)
         finish_inverse(end)
-        flip_res(end - 1)
-        quantise_e(last)
+        flip_last(last)
         deviation(end - 2)
+        quantise_last(last)
         quantise_res(end - 1)
-        inverse_root(end - 2)
-        attend(end)
+        moments(end - 2)
+        attend(end, range(0, NH - 1))
+        attend(end, range(NH - 1, NH))
         project(end - 1)
         flip_res(end)
-        minus_mean(end - 1)
+        centre_v(end - 2)
         quantise_res(end)
         deviation(end - 1)
         finish_v(end - 2, 1)
-        inverse_root(end - 1)
         project(end)
+        moments(end - 1)
         centre_v(end - 1)
-        minus_mean(end)
         deviation(end)
-        finish_v(end - 1, 1)
-        inverse_root(end)
+        moments(end)
         centre_v(end)
+        finish_v(end - 1, 1)
         finish_v(end, 2)

@@ -25,6 +25,8 @@ T_BANKS = T // BANK
 T_PASSES = T // K_PASS
 O_TILES = HID // P
 V_PARTS = 4
+GAMMA_ON_VECTOR = 32
+LAST_LAG = 16
 SCALE = 1.0 / math.sqrt(DH)
 NEG = -10000.0
 EPS = 1e-12
@@ -64,11 +66,16 @@ def tile_multiheadtokenattention_pa_t_kernel(tc, q, k, v, mask, Wo, bo, gamma, b
         beta_all = consts.tile([P, HID], BF16)
         q_rows = q.rearrange("b (n p) f -> p (b n) f", p=P)
         half_tiles = T_TILES // T_BANKS
+        two_heads = 2 * DH
+        half_pairs = T // (4 * P)
         nc.sync.dma_start(out=q_raw[:, 0:1, :], in_=q_rows[:, 0:1, :])
-        nc.sync.dma_start(out=k_raw[0][:, 0:half_tiles, :], in_=k_rows[0][:, 0:half_tiles, :])
-        nc.sync.dma_start(out=k_raw[0][:, half_tiles:, :], in_=k_rows[0][:, half_tiles:, :])
-        nc.sync.dma_start(out=v_raw[0][:], in_=v_rows[0])
-        nc.sync.dma_start(out=q_raw[:, 1:, :], in_=q_rows[:, 1:, :])
+        nc.sync.dma_start(out=k_raw[0][:, 0:half_tiles, 0:two_heads], in_=k_rows[0][:, 0:half_tiles, 0:two_heads])
+        nc.sync.dma_start(out=k_raw[0][:, half_tiles:, 0:two_heads], in_=k_rows[0][:, half_tiles:, 0:two_heads])
+        nc.sync.dma_start(out=k_raw[0][:, :, two_heads:], in_=k_rows[0][:, :, two_heads:])
+        nc.sync.dma_start(out=v_raw[0][:, 0:half_pairs], in_=v_rows[0][:, 0:half_pairs])
+        nc.sync.dma_start(out=q_raw[:, 1:2, :], in_=q_rows[:, 1:2, :])
+        nc.sync.dma_start(out=v_raw[0][:, half_pairs:], in_=v_rows[0][:, half_pairs:])
+        nc.sync.dma_start(out=q_raw[:, 2:, :], in_=q_rows[:, 2:, :])
         nc.sync.dma_start(out=wo_raw[:], in_=Wo.rearrange("(n p) f -> p n f", p=P))
         nc.sync.dma_start(out=bo_all[:], in_=bo.partition_broadcast(P))
         nc.sync.dma_start(out=gamma_all[:], in_=gamma.partition_broadcast(P))
@@ -83,12 +90,10 @@ def tile_multiheadtokenattention_pa_t_kernel(tc, q, k, v, mask, Wo, bo, gamma, b
         make_identity(nc, ident_f32[:])
         minus_half = consts.tile([P, 1], F32)
         nc.vector.memset(minus_half[:], -0.5)
-        zeros = consts.tile([P, 2], F32)
-        nc.vector.memset(zeros[:], 0.0)
-        eps_row = consts.tile([P, 2], F32)
-        nc.vector.tensor_copy(out=eps_row[:, 0:1], in_=zeros[:, 0:1])
+        moments_add = consts.tile([P, 2], F32)
+        nc.vector.memset(moments_add[:], 0.0)
         nc.vector.tensor_scalar(
-            out=eps_row[:, 1:2], in0=zeros[:, 1:2], scalar1=EPS * HID**2, scalar2=None, op0=ALU.add
+            out=moments_add[:, 1:2], in0=moments_add[:, 1:2], scalar1=EPS * HID**2, scalar2=None, op0=ALU.add
         )
         gamma_hid = consts.tile([P, HID], BF16)
 
@@ -147,28 +152,24 @@ def tile_multiheadtokenattention_pa_t_kernel(tc, q, k, v, mask, Wo, bo, gamma, b
                 sentence.tile([P, T_PASSES, HID], U8, tag="v_scales", name="v_scales", align_bytes=64),
             )
 
-        def group_values(s, c):
-            if c == 0:
+        def group_values(s, c, cols, factor):
+            if s not in v_of:
                 new_values(s)
-            nc.gpsimd.tensor_scalar(
-                out=v_of[s][0][:, c].rearrange("p f (u e) -> p f u e", e=2),
-                in0=v_raw[s][:, 2 * c : 2 * c + 2, :].rearrange("p u (e f) -> p f u e", e=2),
-                scalar1=1.0, scalar2=0.0, op0=ALU.mult, op1=ALU.add,
-            )
-
-        def group_values_ahead(s, block):
-            if block == 0:
-                new_values(s)
-            c, eighth = divmod(block, Q_TILES // T_PASSES)
-            width = HID * T_PASSES // Q_TILES
-            cols = slice(eighth * width, (eighth + 1) * width)
-            one = small.tile([P, 1], F32, tag="one")
-            nc.vector.memset(one[:], 1.0)
             nc.gpsimd.tensor_scalar(
                 out=v_of[s][0][:, c, cols].rearrange("p f (u e) -> p f u e", e=2),
                 in0=v_raw[s][:, 2 * c : 2 * c + 2, :].rearrange("p u (e f) -> p f u e", e=2)[:, cols],
-                scalar1=one[:], scalar2=0.0, op0=ALU.mult, op1=ALU.add,
+                scalar1=factor,
+                scalar2=0.0,
+                op0=ALU.mult,
+                op1=ALU.add,
             )
+
+        def group_values_ahead(s, eighth):
+            one = small.tile([P, 1], F32, tag="one")
+            nc.vector.memset(one[:], 1.0)
+            c, part = divmod(eighth, Q_TILES // T_PASSES)
+            width = HID * T_PASSES // Q_TILES
+            group_values(s, c, slice(part * width, (part + 1) * width), one[:])
 
         def quantise_values(s, part):
             grouped, codes, scales = v_of[s]
@@ -293,46 +294,41 @@ def tile_multiheadtokenattention_pa_t_kernel(tc, q, k, v, mask, Wo, bo, gamma, b
             )
             live["e_grouped", i] = grouped
 
-        def flip_last(i):
+        def flip_e_by_pass(i):
             words = live["e", i][:].bitcast(F32)
-            grouped = unit_pool.tile([P, T_PASSES * P * PACK], BF16, tag="e_grouped", name="grouped", align_bytes=64)
-            for c in range(T_PASSES):
-                flipped = psum_tr.tile([P, 2, P], F32, tag="tr", name="flipped")
+            grouped = unit_pool.tile([P, T_PASSES * P * PACK], BF16, tag="e_grouped", align_bytes=64)
+            for c, copy in enumerate((nc.scalar.copy, nc.vector.tensor_copy)):
+                flipped = psum_tr.tile([P, 2, P], F32, tag="tr")
                 for u in range(2):
-                    nc.tensor.transpose(flipped[:, u, :], words[:, (2 * c + u) * P : (2 * c + u + 1) * P], ident_f32[:])
-                (nc.scalar.copy, nc.vector.tensor_copy)[c](
-                    out=grouped[:, c * P * PACK : (c + 1) * P * PACK].bitcast(F32).rearrange("p (r u) -> p r u", u=2),
+                    j = 2 * c + u
+                    nc.tensor.transpose(flipped[:, u, :], words[:, j * P : (j + 1) * P], ident_f32[:])
+                copy(
+                    out=grouped[:, c * K_PASS : (c + 1) * K_PASS].bitcast(F32).rearrange("p (r u) -> p r u", u=2),
                     in_=flipped[:].rearrange("p u r -> p r u"),
                 )
             live["e_grouped", i] = grouped
 
-        def quantise_last(i):
-            codes = packed_pool.tile([P, T_PASSES * P], U32, tag="e_codes", name="codes", align_bytes=64)
-            scales = packed_pool.tile([P, T_PASSES * P], U8, tag="e_scales", name="scales", align_bytes=64)
-            for c in range(T_PASSES):
+        def quantise_e(i, parts=1):
+            codes = packed_pool.tile([P, T_PASSES * P], U32, tag="e_codes", align_bytes=64)
+            scales = packed_pool.tile([P, T_PASSES * P], U8, tag="e_scales", align_bytes=64)
+            width = T_PASSES * P // parts
+            for c in range(parts):
+                cols = slice(c * width, (c + 1) * width)
                 nc.vector.quantize_mx(
-                    out=codes[:, c * P : (c + 1) * P].bitcast(FP8X4), scales=scales[:, c * P : (c + 1) * P],
-                    in_=live["e_grouped", i][:, c * P * PACK : (c + 1) * P * PACK],
+                    out=codes[:, cols].bitcast(FP8X4),
+                    scales=scales[:, cols],
+                    in_=live["e_grouped", i][:, c * width * PACK : (c + 1) * width * PACK],
                 )
             live["e_codes", i] = codes
             live["e_scales", i] = scales
 
-        def quantise_e(i):
-            codes = packed_pool.tile([P, T_PASSES * P], U32, tag="e_codes", align_bytes=64)
-            scales = packed_pool.tile([P, T_PASSES * P], U8, tag="e_scales", align_bytes=64)
-            nc.vector.quantize_mx(
-                out=codes[:].bitcast(FP8X4), scales=scales[:], in_=live["e_grouped", i][:]
-            )
-            live["e_codes", i] = codes
-            live["e_scales", i] = scales
-
-        def invert_sums(n):
+        def add_sums(n):
             by_bank = live["row_sums", n][:].rearrange("p (h b) -> p h b", b=T_BANKS)
             total = small.tile([P, NH], F32, tag="total")
             nc.vector.tensor_tensor(out=total[:], in0=by_bank[:, :, 0], in1=by_bank[:, :, 1], op=ALU.add)
             live["total", n] = total
 
-        def finish_inverse(n):
+        def invert_sums(n):
             inverse = small.tile([P, NH], F32, tag="inverse")
             nc.vector.reciprocal(out=inverse[:], in_=live["total", n][:])
             live["inverse", n] = inverse
@@ -407,157 +403,186 @@ def tile_multiheadtokenattention_pa_t_kernel(tc, q, k, v, mask, Wo, bo, gamma, b
             stats = live["stats", n]
             squares = block_pool.tile([P, HID], BF16, tag="squares")
             nc.scalar.activation(
-                out=squares[:], in_=live["y", n][:], func=ACT.Square, bias=stats[:, 0:1],
-                scale=-1.0 * HID, accum_out=stats[:, 1:2],
+                out=squares[:],
+                in_=live["y", n][:],
+                func=ACT.Square,
+                bias=stats[:, 0:1],
+                scale=-1.0 * HID,
+                accum_out=stats[:, 1:2],
             )
 
-        def moments(n):
+        def moments(n, at_end=False):
             both = small.tile([P, 2], F32, tag="moments")
             nc.vector.scalar_tensor_tensor(
-                out=both[:], in0=live["stats", n][:], scalar=1.0 / HID, in1=eps_row[:], op0=ALU.mult, op1=ALU.add
+                out=both[:],
+                in0=live["stats", n][:],
+                scalar=1.0 / HID,
+                in1=moments_add[:],
+                op0=ALU.mult,
+                op1=ALU.add,
             )
-            rstd = small.tile([P, 1], F32, tag="rstd")
-            nc.gpsimd.tensor_tensor(out=rstd[:], in0=both[:, 1:2], in1=minus_half[:], op=ALU.pow)
-            live["mean", n] = both
-            live["rstd", n] = rstd
+            root = small.tile([P, 1], F32, tag="root")
+            if at_end:
+                nc.scalar.activation(out=root[:], in_=both[:, 1:2], func=ACT.Abs_reciprocal_sqrt)
+            else:
+                nc.gpsimd.tensor_tensor(out=root[:], in0=both[:, 1:2], in1=minus_half[:], op=ALU.pow)
+            live["mean", n] = both[:, 0:1]
+            live["root", n] = root
 
-        def normalise(n, cols):
-            if cols.start == 0:
-                live["normal", n] = block_pool.tile([P, HID], F32, tag="normal", name="normal")
-                live["scaled", n] = block_pool.tile([P, HID], F32, tag="scaled", name="scaled")
-                live["result", n] = block_pool.tile([P, HID], F32, tag="result", name="result")
+        def normalise(n):
+            normal = block_pool.tile([P, HID], F32, tag="normal")
             nc.vector.tensor_scalar(
-                out=live["normal", n][:, cols], in0=live["y", n][:, cols], scalar1=live["mean", n][:, 0:1], scalar2=live["rstd", n][:],
-                op0=ALU.subtract, op1=ALU.mult,
+                out=normal[:],
+                in0=live["y", n][:],
+                scalar1=live["mean", n],
+                scalar2=live["root", n][:],
+                op0=ALU.subtract,
+                op1=ALU.mult,
             )
+            live["normal", n] = normal
 
-        def times_gamma(n, cols):
-            nc.gpsimd.tensor_tensor(
+        def times_gamma(n, engine, cols):
+            if ("scaled", n) not in live:
+                live["scaled", n] = block_pool.tile([P, HID], F32, tag="scaled", name="scaled")
+            engine.tensor_tensor(
                 out=live["scaled", n][:, cols], in0=live["normal", n][:, cols], in1=gamma_hid[:, cols], op=ALU.mult
             )
 
-        def vector_gamma(n, cols):
-            nc.vector.tensor_tensor(
-                out=live["scaled", n][:, cols], in0=live["normal", n][:, cols], in1=gamma_hid[:, cols], op=ALU.mult
-            )
-
-        def plus_beta(n, cols):
-            nc.gpsimd.tensor_tensor(
-                out=live["result", n][:, cols], in0=live["scaled", n][:, cols], in1=beta_all[:, cols], op=ALU.add
-            )
-
-        def store(n):
+        def plus_beta(n):
             s, qt, h = units[n * NH]
-            nc.sync.dma_start(out=out[0, qt * P : (qt + 1) * P, s, :], in_=live["result", n][:])
+            result = block_pool.tile([P, HID], F32, tag="result")
+            nc.gpsimd.tensor_tensor(out=result[:], in0=live["scaled", n][:], in1=beta_all[:], op=ALU.add)
+            nc.sync.dma_start(out=out[0, qt * P : (qt + 1) * P, s, :], in_=result[:])
 
-        def centre_v(n):
-            centred = block_pool.tile([P, HID], F32, tag="scaled", name="centred")
+        def centre(n):
+            centred = block_pool.tile([P, HID], F32, tag="scaled")
             nc.vector.scalar_tensor_tensor(
-                out=centred[:], in0=live["y", n][:], scalar=live["mean", n][:, 0:1], in1=gamma_hid[:],
-                op0=ALU.subtract, op1=ALU.mult,
+                out=centred[:],
+                in0=live["y", n][:],
+                scalar=live["mean", n],
+                in1=gamma_hid[:],
+                op0=ALU.subtract,
+                op1=ALU.mult,
             )
-            live["scaled", n] = centred
+            live["centred", n] = centred
 
-        def finish_v(n, parts):
+        def finish(n, parts=1):
             s, qt, h = units[n * NH]
-            result = block_pool.tile([P, HID], F32, tag="result", name="result")
+            result = block_pool.tile([P, HID], F32, tag="result")
             for i in range(parts):
                 cols = slice(i * HID // parts, (i + 1) * HID // parts)
                 nc.vector.scalar_tensor_tensor(
-                    out=result[:, cols], in0=live["scaled", n][:, cols], scalar=live["rstd", n][:], in1=beta_all[:, cols],
-                    op0=ALU.mult, op1=ALU.add,
+                    out=result[:, cols],
+                    in0=live["centred", n][:, cols],
+                    scalar=live["root", n][:],
+                    in1=beta_all[:, cols],
+                    op0=ALU.mult,
+                    op1=ALU.add,
                 )
                 nc.sync.dma_start(out=out[0, qt * P : (qt + 1) * P, s, cols], in_=result[:, cols])
 
         n_units = len(units)
+        n_blocks = n_units // NH
         per_sentence = Q_TILES * NH
-
-        def at(stage, lag):
-            last = step - lag
-            if 0 <= last < n_units and last % NH == NH - 1:
-                stage(last // NH)
-
+        early = n_blocks - 4
+        gpsimd_cols = slice(0, HID - GAMMA_ON_VECTOR)
+        vector_cols = slice(HID - GAMMA_ON_VECTOR, HID)
         for step in range(n_units):
             s, qt, h = units[step]
             within = step - s * per_sentence
+            due = {}
+            for lag in range(1, LAST_LAG + 1):
+                last_unit = step - lag
+                if last_unit >= 0 and last_unit % NH == NH - 1:
+                    due[lag] = last_unit // NH
+
+            def at(lag, stage, blocks=range(n_blocks)):
+                if due.get(lag) in blocks:
+                    stage(due[lag])
+
             scores(step)
             bank_maxima(step)
-            at(finish_inverse, 4)
+            at(4, invert_sums)
             if step >= 3:
                 quantise_e(step - 3)
             row_shift(step)
-            at(invert_sums, 3)
-            at(quantise_res, 6)
-            at(moments, 9)
-            at(lambda n: normalise(n, slice(0, 512)), 11)
-            at(lambda n: vector_gamma(n, slice(480, 512)), 12)
+            at(3, add_sums)
+            at(6, quantise_res)
+            at(13, moments, range(early))
+            at(9, moments, [early])
+            at(9, centre, [early])
+            at(10, finish, [early])
+            at(15, normalise, range(early))
+            at(16, lambda n: times_gamma(n, nc.vector, vector_cols), range(early))
             if s == 0 and 3 <= within < 3 + V_PARTS:
                 quantise_values(s, within - 3)
             if s > 0 and h < 2 and qt < V_PARTS // 2:
                 quantise_values(s, 2 * qt + h)
-            if h == 1 and s + 1 < S:
+            if s + 1 < S and h == 1:
                 group_values_ahead(s + 1, qt)
-            at(attend, 4)
-            at(project, 7)
-            at(lambda n: times_gamma(n, slice(0, 480)), 11)
-            at(lambda n: plus_beta(n, slice(0, 512)), 12)
-            at(store, 12)
+            at(4, attend)
+            at(7, project)
+            at(15, lambda n: times_gamma(n, nc.gpsimd, gpsimd_cols), range(early))
+            at(16, plus_beta, range(early))
             if step >= 1:
                 exponentials(step - 1)
             if step >= 2:
                 flip_e(step - 2, nc.vector.tensor_copy if step == n_units - 1 else nc.scalar.copy)
-            ahead = within - per_sentence // 2
             if step == 0:
                 transpose_keys(0, 1, 1)
             if s == 0 and within + 2 < NH:
                 for b in range(T_BANKS):
                     transpose_keys(0, within + 2, b)
-            if step == 4:
-                group_wo(0)
-            if step == 5:
-                group_wo(1)
+            if step in (4, 5):
+                group_wo(step - 4)
             if step == 6:
                 quantise_wo()
             if s == 0 and h == 1 and qt + 1 < Q_TILES:
                 transpose_queries(qt + 1)
             if step == 0:
-                group_values(0, 0)
-                group_values(0, 1)
+                for c in range(T_PASSES):
+                    group_values(0, c, slice(0, HID), 1.0)
             if step == 7:
-                nc.vector.tensor_scalar(out=gamma_hid[:], in0=gamma_all[:], scalar1=1.0 * HID, scalar2=None, op0=ALU.mult)
+                nc.vector.tensor_scalar(
+                    out=gamma_hid[:], in0=gamma_all[:], scalar1=1.0 * HID, scalar2=None, op0=ALU.mult
+                )
+            ahead = within - per_sentence // 2
             if s + 1 < S and 0 <= ahead < NH * T_BANKS:
-                transpose_keys(s + 1, ahead // T_BANKS, ahead % T_BANKS, nc.vector.tensor_copy if ahead % 2 == 1 else nc.scalar.copy)
-            at(flip_res, 5)
-            if step < n_units - 1:
-                at(deviation, 8)
+                b = ahead % T_BANKS
+                transpose_keys(s + 1, ahead // T_BANKS, b, nc.vector.tensor_copy if b == 1 else nc.scalar.copy)
+            at(5, flip_res)
+            at(11, deviation, range(early))
+            at(8, deviation, [early])
 
         last = n_units - 1
-        end = n_units // NH - 1
+        end = n_blocks - 1
         exponentials(last)
         flip_e(last - 1, nc.vector.tensor_copy)
         flip_res(end - 1)
-        invert_sums(end)
+        add_sums(end)
         quantise_e(last - 2)
         quantise_e(last - 1)
-        finish_inverse(end)
-        flip_last(last)
+        invert_sums(end)
+        flip_e_by_pass(last)
+        unused = small.tile([P, 1], F32, tag="root")
+        nc.scalar.activation(out=unused[:], in_=minus_half[:], func=ACT.Abs_reciprocal_sqrt)
         deviation(end - 2)
-        quantise_last(last)
+        quantise_e(last, T_PASSES)
         quantise_res(end - 1)
-        moments(end - 2)
         attend(end, range(0, NH - 1))
         attend(end, range(NH - 1, NH))
         project(end - 1)
         flip_res(end)
-        centre_v(end - 2)
+        moments(end - 2, at_end=True)
+        centre(end - 2)
         quantise_res(end)
         deviation(end - 1)
-        finish_v(end - 2, 1)
+        finish(end - 2)
+        moments(end - 1, at_end=True)
         project(end)
-        moments(end - 1)
-        centre_v(end - 1)
+        centre(end - 1)
         deviation(end)
-        moments(end)
-        centre_v(end)
-        finish_v(end - 1, 1)
-        finish_v(end, 2)
+        finish(end - 1)
+        moments(end, at_end=True)
+        centre(end)
+        finish(end, parts=2)

@@ -507,22 +507,24 @@ def tile_multiheadtokenattention_pa_t_kernel(tc, q, k, v, mask, Wo, bo, gamma, b
                 quantise_e(step - 3)
             row_shift(step)
             at(3, add_sums)
-            at(6, quantise_res)
+            at(7, quantise_res, range(early))
+            at(6, quantise_res, range(early, n_blocks))
             at(13, moments, range(early))
             at(9, moments, [early])
             at(9, centre, [early])
             at(10, finish, [early])
-            at(15, normalise, range(early))
+            at(14, normalise, range(early))
             at(16, lambda n: times_gamma(n, nc.vector, vector_cols), range(early))
             if s == 0 and 3 <= within < 3 + V_PARTS:
                 quantise_values(s, within - 3)
-            if s > 0 and h < 2 and qt < V_PARTS // 2:
-                quantise_values(s, 2 * qt + h)
-            if s + 1 < S and h == 1:
+            if s > 0 and h in (0, 2) and qt < V_PARTS // 2:
+                quantise_values(s, 2 * qt + h // 2)
+            if s + 1 < S and h == 2:
                 group_values_ahead(s + 1, qt)
             at(4, attend)
-            at(7, project)
-            at(15, lambda n: times_gamma(n, nc.gpsimd, gpsimd_cols), range(early))
+            at(10, project, range(early))
+            at(7, project, range(early, n_blocks))
+            at(14, lambda n: times_gamma(n, nc.gpsimd, gpsimd_cols), range(early))
             at(16, plus_beta, range(early))
             if step >= 1:
                 exponentials(step - 1)
@@ -537,7 +539,7 @@ def tile_multiheadtokenattention_pa_t_kernel(tc, q, k, v, mask, Wo, bo, gamma, b
                 group_wo(step - 4)
             if step == 6:
                 quantise_wo()
-            if s == 0 and h == 1 and qt + 1 < Q_TILES:
+            if s == 0 and h == 2 and qt + 1 < Q_TILES:
                 transpose_queries(qt + 1)
             if step == 0:
                 for c in range(T_PASSES):
@@ -546,10 +548,9 @@ def tile_multiheadtokenattention_pa_t_kernel(tc, q, k, v, mask, Wo, bo, gamma, b
                 nc.vector.tensor_scalar(
                     out=gamma_hid[:], in0=gamma_all[:], scalar1=1.0 * HID, scalar2=None, op0=ALU.mult
                 )
-            ahead = within - per_sentence // 2
-            if s + 1 < S and 0 <= ahead < NH * T_BANKS:
-                b = ahead % T_BANKS
-                transpose_keys(s + 1, ahead // T_BANKS, b, nc.vector.tensor_copy if b == 1 else nc.scalar.copy)
+            if s + 1 < S and qt >= Q_TILES // 2 and h % 2 == 1:
+                b = h // 2
+                transpose_keys(s + 1, qt - Q_TILES // 2, b, nc.vector.tensor_copy if b == 1 else nc.scalar.copy)
             at(5, flip_res)
             at(11, deviation, range(early))
             at(8, deviation, [early])
@@ -585,4 +586,4 @@ def tile_multiheadtokenattention_pa_t_kernel(tc, q, k, v, mask, Wo, bo, gamma, b
         finish(end - 1)
         moments(end, at_end=True)
         centre(end)
-        finish(end, parts=2)
+        finish(end, parts=4)

from contextlib import ExitStack
import math

import concourse.mybir as mybir
from concourse.masks import make_identity

F32 = mybir.dt.float32
BF16 = mybir.dt.bfloat16
U32 = mybir.dt.uint32
U8 = mybir.dt.uint8
FP8X4 = mybir.dt.float8_e4m3fn_x4
ALU = mybir.AluOpType
ACT = mybir.ActivationFunctionType
AX = mybir.AxisListType

Q, S, T, HID, NH = 1024, 4, 1024, 512, 4
DH = HID // NH
P = 128
PACK = 4
K_PASS = P * PACK
BANK = 512
Q_TILES = Q // P
T_TILES = T // P
T_BANKS = T // BANK
T_PASSES = T // K_PASS
O_TILES = HID // P
V_PARTS = 4
GAMMA_ON_VECTOR = 32
LAST_LAG = 16
SCALE = 1.0 / math.sqrt(DH)
NEG = -10000.0
EPS = 1e-12

FLOPS = 2 * S * NH * Q * T * DH * 2 + 2 * Q * S * HID * HID


def tile_multiheadtokenattention_pa_t_kernel(tc, q, k, v, mask, Wo, bo, gamma, beta, out):
    nc = tc.nc
    with ExitStack() as stack:
        stack.enter_context(tc.manual_schedule())
        consts = stack.enter_context(tc.tile_pool(name="consts", bufs=1))
        sentence = stack.enter_context(tc.tile_pool(name="sentence", bufs=2))
        unit_pool = stack.enter_context(tc.tile_pool(name="unit", bufs=3))
        packed_pool = stack.enter_context(tc.tile_pool(name="packed", bufs=2 * NH))
        block_pool = stack.enter_context(tc.tile_pool(name="block", bufs=3))
        small = stack.enter_context(tc.tile_pool(name="small", bufs=6))
        psum_sc = stack.enter_context(tc.psum_pool(name="psum_sc", bufs=5))
        psum_tr = stack.enter_context(tc.psum_pool(name="psum_tr", bufs=3))

        mask_rows = consts.tile([P, P], BF16)
        nc.vector.memset(mask_rows[:], 0.0)
        nc.sync.dma_start(
            out=mask_rows[0 : S * T_TILES, :], in_=mask.rearrange("b s (c t) -> (b s c) t", t=P)
        )
        k_rows = k.rearrange("b s (n p) f -> (b s) p n f", p=P)
        v_rows = v.rearrange("b s (j p e) f -> (b s) p j (e f)", p=P, e=2)
        k_raw = []
        v_raw = []
        for s in range(S):
            k_raw.append(consts.tile([P, T_TILES, HID], BF16, name="k_raw%d" % s))
            v_raw.append(consts.tile([P, T // (2 * P), 2 * HID], BF16, name="v_raw%d" % s))
        q_raw = consts.tile([P, Q_TILES, HID], BF16)
        wo_raw = consts.tile([P, O_TILES, HID], BF16)
        bo_all = consts.tile([P, HID], BF16)
        gamma_all = consts.tile([P, HID], BF16)
        beta_all = consts.tile([P, HID], BF16)
        q_rows = q.rearrange("b (n p) f -> p (b n) f", p=P)
        half_tiles = T_TILES // T_BANKS
        two_heads = 2 * DH
        half_pairs = T // (4 * P)
        nc.sync.dma_start(out=q_raw[:, 0:1, :], in_=q_rows[:, 0:1, :])
        nc.sync.dma_start(out=k_raw[0][:, 0:half_tiles, 0:two_heads], in_=k_rows[0][:, 0:half_tiles, 0:two_heads])
        nc.sync.dma_start(out=k_raw[0][:, half_tiles:, 0:two_heads], in_=k_rows[0][:, half_tiles:, 0:two_heads])
        nc.sync.dma_start(out=k_raw[0][:, :, two_heads:], in_=k_rows[0][:, :, two_heads:])
        nc.sync.dma_start(out=v_raw[0][:, 0:half_pairs], in_=v_rows[0][:, 0:half_pairs])
        nc.sync.dma_start(out=q_raw[:, 1:2, :], in_=q_rows[:, 1:2, :])
        nc.sync.dma_start(out=v_raw[0][:, half_pairs:], in_=v_rows[0][:, half_pairs:])
        nc.sync.dma_start(out=q_raw[:, 2:, :], in_=q_rows[:, 2:, :])
        nc.sync.dma_start(out=wo_raw[:], in_=Wo.rearrange("(n p) f -> p n f", p=P))
        nc.sync.dma_start(out=bo_all[:], in_=bo.partition_broadcast(P))
        nc.sync.dma_start(out=gamma_all[:], in_=gamma.partition_broadcast(P))
        nc.sync.dma_start(out=beta_all[:], in_=beta.partition_broadcast(P))
        for s in range(1, S):
            nc.sync.dma_start(out=v_raw[s][:], in_=v_rows[s])
            nc.sync.dma_start(out=k_raw[s][:], in_=k_rows[s])

        ident_bf = consts.tile([P, P], BF16)
        make_identity(nc, ident_bf[:])
        ident_f32 = consts.tile([P, P], F32)
        make_identity(nc, ident_f32[:])
        minus_half = consts.tile([P, 1], F32)
        nc.vector.memset(minus_half[:], -0.5)
        moments_add = consts.tile([P, 2], F32)
        nc.vector.memset(moments_add[:], 0.0)
        nc.vector.tensor_scalar(
            out=moments_add[:, 1:2], in0=moments_add[:, 1:2], scalar1=EPS * HID**2, scalar2=None, op0=ALU.add
        )
        gamma_hid = consts.tile([P, HID], BF16)

        mask_flipped = psum_tr.tile([P, P], BF16, tag="tr")
        nc.tensor.transpose(mask_flipped[:], mask_rows[:], ident_bf[:])
        mask_col = consts.tile([P, S * T_TILES], F32)
        nc.vector.tensor_scalar(
            out=mask_col[:],
            in0=mask_flipped[:, 0 : S * T_TILES],
            scalar1=NEG / SCALE,
            scalar2=None,
            op0=ALU.mult,
        )
        mask_bias = consts.tile([P, S * T_TILES, P], F32)

        def spread_mask(s):
            tiles = slice(s * T_TILES, (s + 1) * T_TILES)
            nc.vector.tensor_copy(
                out=mask_bias[:, tiles, :],
                in_=mask_col[:, tiles].unsqueeze(2).to_broadcast([P, T_TILES, P]),
            )

        spread_mask(0)

        qT = consts.tile([P, NH, Q], BF16)
        kT_of = {}
        v_of = {}

        def transpose_queries(qt):
            flipped = psum_tr.tile([P, NH, P], BF16, tag="tr")
            for h in range(NH):
                nc.tensor.transpose(
                    flipped[:, h, :], q_raw[:, qt, h * DH : (h + 1) * DH], ident_bf[:]
                )
            nc.vector.tensor_copy(out=qT[:, :, qt * P : (qt + 1) * P], in_=flipped[:])

        def transpose_keys(s, h, b, copy=nc.scalar.copy):
            if h == 0 and b == 0:
                kT_of[s] = sentence.tile([P, NH, T], BF16, tag="kT", name="kT")
            flipped = psum_tr.tile([P, half_tiles, P], BF16, tag="tr")
            for j in range(half_tiles):
                nc.tensor.transpose(
                    flipped[:, j, :],
                    k_raw[s][:, b * half_tiles + j, h * DH : (h + 1) * DH],
                    ident_bf[:],
                )
            copy(
                out=kT_of[s][:, h, b * BANK : (b + 1) * BANK],
                in_=flipped[:].rearrange("p j t -> p (j t)"),
            )

        def new_values(s):
            v_of[s] = (
                sentence.tile([P, T_PASSES, HID, PACK], BF16, tag="v_grouped", name="v_grouped", align_bytes=64),
                sentence.tile([P, T_PASSES, HID], U32, tag="v_codes", name="v_codes", align_bytes=64),
                sentence.tile([P, T_PASSES, HID], U8, tag="v_scales", name="v_scales", align_bytes=64),
            )

        def group_values(s, c, cols, factor):
            if s not in v_of:
                new_values(s)
            nc.gpsimd.tensor_scalar(
                out=v_of[s][0][:, c, cols].rearrange("p f (u e) -> p f u e", e=2),
                in0=v_raw[s][:, 2 * c : 2 * c + 2, :].rearrange("p u (e f) -> p f u e", e=2)[:, cols],
                scalar1=factor,
                scalar2=0.0,
                op0=ALU.mult,
                op1=ALU.add,
            )

        def group_values_ahead(s, eighth):
            one = small.tile([P, 1], F32, tag="one")
            nc.vector.memset(one[:], 1.0)
            c, part = divmod(eighth, Q_TILES // T_PASSES)
            width = HID * T_PASSES // Q_TILES
            group_values(s, c, slice(part * width, (part + 1) * width), one[:])

        def quantise_values(s, part):
            grouped, codes, scales = v_of[s]
            c, half = divmod(part, 2)
            cols = slice(half * HID // 2, (half + 1) * HID // 2)
            nc.vector.quantize_mx(
                out=codes[:, c, cols].bitcast(FP8X4),
                scales=scales[:, c, cols],
                in_=grouped[:, c, cols].rearrange("p f j -> p (f j)"),
            )

        wo_grouped = consts.tile([P, HID, PACK], BF16, align_bytes=64)
        wo_codes = consts.tile([P, HID], U32, align_bytes=64)
        wo_scales = consts.tile([P, HID], U8, align_bytes=64)

        def group_wo(half):
            wo_words = wo_raw[:].bitcast(F32)
            wo_grouped_words = wo_grouped[:].bitcast(F32)
            flipped = psum_tr.tile([P, 2, 2, P], F32, tag="tr")
            for a in range(2):
                for u in range(2):
                    nc.tensor.transpose(
                        flipped[:, a, u, :],
                        wo_words[:, 2 * half + a, u * P : (u + 1) * P],
                        ident_f32[:],
                    )
            nc.scalar.copy(
                out=wo_grouped_words[:, 2 * half * P : (2 * half + 2) * P, :].rearrange(
                    "p (a o) u -> p a o u", a=2
                ),
                in_=flipped[:].rearrange("p a u o -> p a o u"),
            )

        def quantise_wo():
            nc.vector.quantize_mx(
                out=wo_codes[:].bitcast(FP8X4),
                scales=wo_scales[:],
                in_=wo_grouped[:].rearrange("p o j -> p (o j)"),
            )

        transpose_queries(0)
        transpose_keys(0, 0, 0)
        transpose_keys(0, 1, 0, nc.vector.tensor_copy)
        transpose_keys(0, 0, 1)
        for s in range(1, S):
            spread_mask(s)

        units = [(s, qt, h) for s in range(S) for qt in range(Q_TILES) for h in range(NH)]
        live = {}

        def scores(i):
            s, qt, h = units[i]
            for b in range(T_BANKS):
                sc = psum_sc.tile([P, BANK], F32, tag="sc")
                for j in range(BANK // P):
                    nc.tensor.matmul(
                        out=sc[:, j * P : (j + 1) * P],
                        lhsT=mask_bias[:, s * T_TILES + b * (BANK // P) + j, :],
                        rhs=ident_f32[:],
                        is_transpose=True,
                        start=(j == 0),
                        stop=False,
                    )
                nc.tensor.matmul(
                    out=sc[:],
                    lhsT=qT[:, h, qt * P : (qt + 1) * P],
                    rhs=kT_of[s][:, h, b * BANK : (b + 1) * BANK],
                    start=False,
                    stop=True,
                )
                live["sc", i, b] = sc

        def bank_maxima(i):
            top = small.tile([P, T_BANKS], F32, tag="top")
            for b in range(T_BANKS):
                nc.vector.tensor_reduce(
                    out=top[:, b : b + 1], in_=live["sc", i, b][:], axis=AX.X, op=ALU.max
                )
            live["top", i] = top

        def row_shift(i):
            top = live["top", i]
            shift = small.tile([P, 1], F32, tag="shift")
            nc.vector.tensor_scalar(
                out=shift[:],
                in0=top[:, 0:1],
                scalar1=top[:, 1:2],
                scalar2=-SCALE,
                op0=ALU.max,
                op1=ALU.mult,
            )
            live["shift", i] = shift

        def exponentials(i):
            h = units[i][2]
            if h == 0:
                live["row_sums", i // NH] = small.tile(
                    [P, NH * T_BANKS], F32, tag="row_sums", name="row_sums"
                )
            row_sums = live["row_sums", i // NH]
            e = unit_pool.tile([P, T], BF16, tag="e")
            for b in range(T_BANKS):
                nc.scalar.activation(
                    out=e[:, b * BANK : (b + 1) * BANK],
                    in_=live["sc", i, b][:],
                    func=ACT.Exp,
                    bias=live["shift", i][:],
                    scale=SCALE,
                    accum_out=row_sums[:, h * T_BANKS + b : h * T_BANKS + b + 1],
                )
            live["e", i] = e

        def flip_e(i, copy=nc.scalar.copy):
            words = live["e", i][:].bitcast(F32)
            flipped = psum_tr.tile([P, T_PASSES * 2, P], F32, tag="tr")
            for j in range(T_PASSES * 2):
                nc.tensor.transpose(flipped[:, j, :], words[:, j * P : (j + 1) * P], ident_f32[:])
            grouped = unit_pool.tile([P, T_PASSES * P * PACK], BF16, tag="e_grouped", align_bytes=64)
            copy(
                out=grouped[:].bitcast(F32).rearrange("p (c r u) -> p c r u", c=T_PASSES, u=2),
                in_=flipped[:].rearrange("p (c u) r -> p c r u", u=2),
            )
            live["e_grouped", i] = grouped

        def flip_e_by_pass(i):
            words = live["e", i][:].bitcast(F32)
            grouped = unit_pool.tile([P, T_PASSES * P * PACK], BF16, tag="e_grouped", align_bytes=64)
            for c, copy in enumerate((nc.scalar.copy, nc.vector.tensor_copy)):
                flipped = psum_tr.tile([P, 2, P], F32, tag="tr")
                for u in range(2):
                    j = 2 * c + u
                    nc.tensor.transpose(flipped[:, u, :], words[:, j * P : (j + 1) * P], ident_f32[:])
                copy(
                    out=grouped[:, c * K_PASS : (c + 1) * K_PASS].bitcast(F32).rearrange("p (r u) -> p r u", u=2),
                    in_=flipped[:].rearrange("p u r -> p r u"),
                )
            live["e_grouped", i] = grouped

        def quantise_e(i, parts=1):
            codes = packed_pool.tile([P, T_PASSES * P], U32, tag="e_codes", align_bytes=64)
            scales = packed_pool.tile([P, T_PASSES * P], U8, tag="e_scales", align_bytes=64)
            width = T_PASSES * P // parts
            for c in range(parts):
                cols = slice(c * width, (c + 1) * width)
                nc.vector.quantize_mx(
                    out=codes[:, cols].bitcast(FP8X4),
                    scales=scales[:, cols],
                    in_=live["e_grouped", i][:, c * width * PACK : (c + 1) * width * PACK],
                )
            live["e_codes", i] = codes
            live["e_scales", i] = scales

        def add_sums(n):
            by_bank = live["row_sums", n][:].rearrange("p (h b) -> p h b", b=T_BANKS)
            total = small.tile([P, NH], F32, tag="total")
            nc.vector.tensor_tensor(out=total[:], in0=by_bank[:, :, 0], in1=by_bank[:, :, 1], op=ALU.add)
            live["total", n] = total

        def invert_sums(n):
            inverse = small.tile([P, NH], F32, tag="inverse")
            nc.vector.reciprocal(out=inverse[:], in_=live["total", n][:])
            live["inverse", n] = inverse

        def attend(n, heads=range(NH)):
            s = units[n * NH][0]
            v_codes, v_scales = v_of[s][1], v_of[s][2]
            ctx_ps = psum_tr.tile([P, HID], F32, tag="tr")
            if heads[0] == 0:
                live["res", n] = block_pool.tile([P, HID], BF16, tag="res", name="res")
            for h in heads:
                for c in range(T_PASSES):
                    nc.tensor.matmul_mx(
                        out=ctx_ps[:, h * DH : (h + 1) * DH],
                        lhsT=live["e_codes", n * NH + h][:, c * P : (c + 1) * P].bitcast(FP8X4),
                        lhsT_scale=live["e_scales", n * NH + h][:, c * P : (c + 1) * P],
                        rhs=v_codes[:, c, h * DH : (h + 1) * DH].bitcast(FP8X4),
                        rhs_scale=v_scales[:, c, h * DH : (h + 1) * DH],
                        start=(c == 0),
                        stop=(c == T_PASSES - 1),
                    )
            cols = slice(heads[0] * DH, (heads[-1] + 1) * DH)
            nc.vector.tensor_tensor(
                out=live["res", n][:, cols].rearrange("p (h d) -> p h d", d=DH),
                in0=ctx_ps[:, cols].rearrange("p (h d) -> p h d", d=DH),
                in1=live["inverse", n][:, heads[0] : heads[-1] + 1].unsqueeze(2).to_broadcast([P, len(heads), DH]),
                op=ALU.mult,
            )

        def flip_res(n):
            words = live["res", n][:].bitcast(F32)
            flipped = psum_tr.tile([P, 2, P], F32, tag="tr")
            for u in range(2):
                nc.tensor.transpose(flipped[:, u, :], words[:, u * P : (u + 1) * P], ident_f32[:])
            grouped = block_pool.tile([P, P * PACK], BF16, tag="res_grouped", align_bytes=64)
            nc.scalar.copy(
                out=grouped[:].bitcast(F32).rearrange("p (r u) -> p r u", u=2),
                in_=flipped[:].rearrange("p u r -> p r u"),
            )
            live["res_grouped", n] = grouped

        def quantise_res(n):
            codes = block_pool.tile([P, P], U32, tag="res_codes", align_bytes=64)
            scales = block_pool.tile([P, P], U8, tag="res_scales", align_bytes=64)
            nc.vector.quantize_mx(
                out=codes[:].bitcast(FP8X4), scales=scales[:], in_=live["res_grouped", n][:]
            )
            live["res_codes", n] = codes
            live["res_scales", n] = scales

        def project(n):
            y_ps = psum_tr.tile([P, HID], F32, tag="tr")
            nc.tensor.matmul_mx(
                out=y_ps[:],
                lhsT=live["res_codes", n][:].bitcast(FP8X4),
                lhsT_scale=live["res_scales", n][:],
                rhs=wo_codes[:].bitcast(FP8X4),
                rhs_scale=wo_scales[:],
                start=True,
                stop=True,
            )
            y = block_pool.tile([P, HID], F32, tag="y_sb")
            stats = small.tile([P, 2], F32, tag="stats")
            nc.vector.scalar_tensor_tensor(
                out=y[:], in0=y_ps[:], scalar=1.0, in1=bo_all[:], op0=ALU.mult, op1=ALU.add,
                accum_out=stats[:, 0:1],
            )
            live["y", n] = y
            live["stats", n] = stats

        def deviation(n):
            stats = live["stats", n]
            squares = block_pool.tile([P, HID], BF16, tag="squares")
            nc.scalar.activation(
                out=squares[:],
                in_=live["y", n][:],
                func=ACT.Square,
                bias=stats[:, 0:1],
                scale=-1.0 * HID,
                accum_out=stats[:, 1:2],
            )

        def moments(n, at_end=False):
            both = small.tile([P, 2], F32, tag="moments")
            nc.vector.scalar_tensor_tensor(
                out=both[:],
                in0=live["stats", n][:],
                scalar=1.0 / HID,
                in1=moments_add[:],
                op0=ALU.mult,
                op1=ALU.add,
            )
            root = small.tile([P, 1], F32, tag="root")
            if at_end:
                nc.scalar.activation(out=root[:], in_=both[:, 1:2], func=ACT.Abs_reciprocal_sqrt)
            else:
                nc.gpsimd.tensor_tensor(out=root[:], in0=both[:, 1:2], in1=minus_half[:], op=ALU.pow)
            live["mean", n] = both[:, 0:1]
            live["root", n] = root

        def normalise(n):
            normal = block_pool.tile([P, HID], F32, tag="normal")
            nc.vector.tensor_scalar(
                out=normal[:],
                in0=live["y", n][:],
                scalar1=live["mean", n],
                scalar2=live["root", n][:],
                op0=ALU.subtract,
                op1=ALU.mult,
            )
            live["normal", n] = normal

        def times_gamma(n, engine, cols):
            if ("scaled", n) not in live:
                live["scaled", n] = block_pool.tile([P, HID], F32, tag="scaled", name="scaled")
            engine.tensor_tensor(
                out=live["scaled", n][:, cols], in0=live["normal", n][:, cols], in1=gamma_hid[:, cols], op=ALU.mult
            )

        def plus_beta(n):
            s, qt, h = units[n * NH]
            result = block_pool.tile([P, HID], F32, tag="result")
            nc.gpsimd.tensor_tensor(out=result[:], in0=live["scaled", n][:], in1=beta_all[:], op=ALU.add)
            nc.sync.dma_start(out=out[0, qt * P : (qt + 1) * P, s, :], in_=result[:])

        def centre(n):
            centred = block_pool.tile([P, HID], F32, tag="scaled")
            nc.vector.scalar_tensor_tensor(
                out=centred[:],
                in0=live["y", n][:],
                scalar=live["mean", n],
                in1=gamma_hid[:],
                op0=ALU.subtract,
                op1=ALU.mult,
            )
            live["centred", n] = centred

        def finish(n, parts=1):
            s, qt, h = units[n * NH]
            result = block_pool.tile([P, HID], F32, tag="result")
            for i in range(parts):
                cols = slice(i * HID // parts, (i + 1) * HID // parts)
                nc.vector.scalar_tensor_tensor(
                    out=result[:, cols],
                    in0=live["centred", n][:, cols],
                    scalar=live["root", n][:],
                    in1=beta_all[:, cols],
                    op0=ALU.mult,
                    op1=ALU.add,
                )
                nc.sync.dma_start(out=out[0, qt * P : (qt + 1) * P, s, cols], in_=result[:, cols])

        n_units = len(units)
        n_blocks = n_units // NH
        per_sentence = Q_TILES * NH
        early = n_blocks - 4
        gpsimd_cols = slice(0, HID - GAMMA_ON_VECTOR)
        vector_cols = slice(HID - GAMMA_ON_VECTOR, HID)
        for step in range(n_units):
            s, qt, h = units[step]
            within = step - s * per_sentence
            due = {}
            for lag in range(1, LAST_LAG + 1):
                last_unit = step - lag
                if last_unit >= 0 and last_unit % NH == NH - 1:
                    due[lag] = last_unit // NH

            def at(lag, stage, blocks=range(n_blocks)):
                if due.get(lag) in blocks:
                    stage(due[lag])

            scores(step)
            bank_maxima(step)
            at(4, invert_sums)
            if step >= 3:
                quantise_e(step - 3)
            row_shift(step)
            at(3, add_sums)
            at(7, quantise_res, range(early))
            at(6, quantise_res, range(early, n_blocks))
            at(13, moments, range(early))
            at(9, moments, [early])
            at(9, centre, [early])
            at(10, finish, [early])
            at(14, normalise, range(early))
            at(16, lambda n: times_gamma(n, nc.vector, vector_cols), range(early))
            if s == 0 and 3 <= within < 3 + V_PARTS:
                quantise_values(s, within - 3)
            if s > 0 and h in (0, 2) and qt < V_PARTS // 2:
                quantise_values(s, 2 * qt + h // 2)
            if s + 1 < S and h == 2:
                group_values_ahead(s + 1, qt)
            at(4, attend)
            at(10, project, range(early))
            at(7, project, range(early, n_blocks))
            at(14, lambda n: times_gamma(n, nc.gpsimd, gpsimd_cols), range(early))
            at(16, plus_beta, range(early))
            if step >= 1:
                exponentials(step - 1)
            if step >= 2:
                flip_e(step - 2, nc.vector.tensor_copy if step == n_units - 1 else nc.scalar.copy)
            if step == 0:
                transpose_keys(0, 1, 1)
            if s == 0 and within + 2 < NH:
                for b in range(T_BANKS):
                    transpose_keys(0, within + 2, b)
            if step in (4, 5):
                group_wo(step - 4)
            if step == 6:
                quantise_wo()
            if s == 0 and h == 2 and qt + 1 < Q_TILES:
                transpose_queries(qt + 1)
            if step == 0:
                for c in range(T_PASSES):
                    group_values(0, c, slice(0, HID), 1.0)
            if step == 7:
                nc.vector.tensor_scalar(
                    out=gamma_hid[:], in0=gamma_all[:], scalar1=1.0 * HID, scalar2=None, op0=ALU.mult
                )
            if s + 1 < S and qt >= Q_TILES // 2 and h % 2 == 1:
                b = h // 2
                transpose_keys(s + 1, qt - Q_TILES // 2, b, nc.vector.tensor_copy if b == 1 else nc.scalar.copy)
            at(5, flip_res)
            at(11, deviation, range(early))
            at(8, deviation, [early])

        last = n_units - 1
        end = n_blocks - 1
        exponentials(last)
        flip_e(last - 1, nc.vector.tensor_copy)
        flip_res(end - 1)
        add_sums(end)
        quantise_e(last - 2)
        quantise_e(last - 1)
        invert_sums(end)
        flip_e_by_pass(last)
        unused = small.tile([P, 1], F32, tag="root")
        nc.scalar.activation(out=unused[:], in_=minus_half[:], func=ACT.Abs_reciprocal_sqrt)
        deviation(end - 2)
        quantise_e(last, T_PASSES)
        quantise_res(end - 1)
        attend(end, range(0, NH - 1))
        attend(end, range(NH - 1, NH))
        project(end - 1)
        flip_res(end)
        moments(end - 2, at_end=True)
        centre(end - 2)
        quantise_res(end)
        deviation(end - 1)
        finish(end - 2)
        moments(end - 1, at_end=True)
        project(end)
        centre(end - 1)
        deviation(end)
        finish(end - 1)
        moments(end, at_end=True)
        centre(end)
        finish(end, parts=4)
